import numpy as np
import ml_dtypes


def mxq(x, axis, fmt="e4m3"):
    dtype, down = {"e4m3": (ml_dtypes.float8_e4m3fn, 7), "e5m2": (ml_dtypes.float8_e5m2, 14)}[fmt]
    v = np.moveaxis(np.asarray(x, np.float32).astype(ml_dtypes.bfloat16).astype(np.float64), axis, -1)
    blocks = v.reshape(v.shape[:-1] + (-1, 32))
    amax = np.abs(blocks).max(-1, keepdims=True)
    byte = np.maximum(np.where(amax > 0, np.frexp(amax)[1] - 1 + 127, 0) - down, 1)
    scale = np.exp2(byte - 127.0)
    codes = (blocks / scale).astype(np.float32).astype(dtype).astype(np.float64)
    return np.moveaxis((codes * scale).reshape(v.shape), -1, axis)


WIDE = False


def mx_kscale(k):
    if not WIDE:
        return np.ones(k)
    levels = np.array([10, -10, 5, -5, 0])
    a = np.random.permutation(np.resize(levels, k // 512 * 4)).reshape(k // 512, 4)
    idx = np.arange(k)
    return np.exp2(a[idx // 512, idx % 128 // 32])


BF16 = ml_dtypes.bfloat16


def bf(x):
    return np.asarray(x, np.float32).astype(BF16)


def f64(x):
    return np.asarray(x).astype(np.float64)


E2M1 = np.array([0.0, 0.5, 1.0, 1.5, 2.0, 3.0, 4.0, 6.0, -0.0, -0.5, -1.0, -1.5, -2.0, -3.0, -4.0, -6.0])


def pack_weight(w, fmt):
    k, n = w.shape
    w = f64(bf(w)).reshape(k // 32, 32, n)
    amax = np.abs(w).max(1)
    if fmt == "e4m3":
        byte = np.frexp(amax)[1] - 1 + 127 - 7
    else:
        mant, ex = np.frexp(amax / 6.0)
        byte = np.where(mant > 0.5, ex, ex - 1) + 127
    byte = np.clip(np.where(amax > 0, byte, 1), 1, 254)
    scaled = (w * np.exp2(127.0 - byte)[:, None, :]).reshape(k, n).astype(np.float32)
    by_word = np.ascontiguousarray(scaled.reshape(k // 512, 128, 4, n).transpose(0, 1, 3, 2))
    if fmt == "e4m3":
        words = by_word.astype(ml_dtypes.float8_e4m3fn).view(np.uint8)
    else:
        c = by_word.astype(ml_dtypes.float4_e2m1fn).view(np.uint8) & 0xF
        words = c[..., 0::2] | (c[..., 1::2] << 4)
    return np.ascontiguousarray(words), np.ascontiguousarray(byte.astype(np.uint8).reshape(k // 512, 16, n))


def unpack_weight(words, scales, fmt):
    g, p, n, _ = words.shape
    if fmt == "e4m3":
        vals = np.ascontiguousarray(words).view(ml_dtypes.float8_e4m3fn).astype(np.float64)
    else:
        nib = np.empty((g, p, n, 4), np.uint8)
        nib[..., 0::2] = words & 0xF
        nib[..., 1::2] = words >> 4
        vals = E2M1[nib]
    vals = vals * np.repeat(np.exp2(scales.astype(np.float64) - 127.0), 8, axis=1)[..., None]
    return vals.transpose(0, 1, 3, 2).reshape(g * 512, n)


B, L, D, F = 2, 512, 1024, 1536
FMT = "e4m3"


def silu(z):
    return z / (1.0 + np.exp(-z))


def sigmoid(z):
    return 1.0 / (1.0 + np.exp(-z))


def setup_inputs():
    s = mx_kscale(D)
    x = bf(np.random.standard_normal((B, L, D)) * s)
    W1_words, W1_scales = pack_weight(np.random.standard_normal((D, F)) / np.sqrt(D) / s[:, None], FMT)
    b1 = bf(np.random.standard_normal(F) * 0.3)
    W2g_words, W2g_scales = pack_weight(np.random.standard_normal((F, D)) * 2.4 / np.sqrt(F), FMT)
    b2g = bf(np.random.standard_normal(D) * 0.3)
    Wv_words, Wv_scales = pack_weight(np.random.standard_normal((D, D)) * 1.8 / np.sqrt(D) / s[:, None], FMT)
    bv = bf(np.random.standard_normal(D) * 0.3)
    return {
        "x": x,
        "W1_words": W1_words,
        "W1_scales": W1_scales,
        "b1": b1,
        "W2g_words": W2g_words,
        "W2g_scales": W2g_scales,
        "b2g": b2g,
        "Wv_words": Wv_words,
        "Wv_scales": Wv_scales,
        "bv": bv,
    }


def reference(x, W1_words, W1_scales, b1, W2g_words, W2g_scales, b2g, Wv_words, Wv_scales, bv):
    xq = mxq(f64(x), 2, "e4m3")
    h = silu((xq @ unpack_weight(W1_words, W1_scales, FMT)) + f64(b1))
    g = (mxq(h, 2, "e4m3") @ unpack_weight(W2g_words, W2g_scales, FMT)) + f64(b2g)
    return ((xq @ unpack_weight(Wv_words, Wv_scales, FMT)) + f64(bv)) * sigmoid(g)

@@ -1,0 +1,279 @@
+from contextlib import ExitStack
+
+import concourse.mybir as mybir
+from concourse.masks import make_identity
+
+F32 = mybir.dt.float32
+BF16 = mybir.dt.bfloat16
+I32 = mybir.dt.int32
+U8 = mybir.dt.uint8
+FP8X4 = mybir.dt.float8_e4m3fn_x4
+ACT = mybir.ActivationFunctionType
+ALU = mybir.AluOpType
+
+P = 128
+PACK = 4
+K_PASS = P * PACK
+TOKENS = 1024
+D_MODEL = 1024
+D_HIDDEN = 1536
+CHUNK = 512
+N_CHUNKS = TOKENS // CHUNK
+TOKEN_TILES = CHUNK // P
+X_PASSES = D_MODEL // K_PASS
+H_PASSES = D_HIDDEN // K_PASS
+UNIT_TILES = K_PASS // P
+OUT_TILES = D_MODEL // P
+BLOCK = CHUNK // P
+QUADRANTS = 4
+BLOCKS = OUT_TILES // BLOCK
+B1_COL = 0
+B2G_COL = B1_COL + D_HIDDEN // P
+BV_COL = B2G_COL + OUT_TILES
+
+FLOPS = 2 * TOKENS * (D_MODEL * D_HIDDEN + D_HIDDEN * D_MODEL + D_MODEL * D_MODEL)
+
+
+def tile_selectivemixing_pa_kernel(
+    tc, x, W1_words, W1_scales, b1, W2g_words, W2g_scales, b2g, Wv_words, Wv_scales, bv, out
+):
+    nc = tc.nc
+    x_rows = x.rearrange("b l d -> (b l) d")
+    out_rows = out.rearrange("b l d -> (b l) d")
+    park_rows = out_rows.bitcast(BF16)
+
+    with ExitStack() as ctx:
+        ctx.enter_context(tc.manual_schedule())
+        keep = ctx.enter_context(tc.tile_pool(name="keep", bufs=1))
+        stage = ctx.enter_context(tc.tile_pool(name="stage", bufs=3))
+        mixing = ctx.enter_context(tc.tile_pool(name="mixing", bufs=BLOCK + 2))
+        results = ctx.enter_context(tc.tile_pool(name="results", bufs=2 * TOKEN_TILES))
+        sums = ctx.enter_context(tc.psum_pool(name="sums", bufs=4))
+        flipped = ctx.enter_context(tc.psum_pool(name="flipped", bufs=4))
+
+        w1_planes = keep.tile([P, D_HIDDEN], U8, align_bytes=64)
+        w2_planes = keep.tile([P, D_MODEL], U8, align_bytes=64)
+        wv_planes = keep.tile([P, D_MODEL], U8, align_bytes=64)
+        bias_rows = keep.tile([P, P], BF16)
+        nc.vector.memset(w1_planes[:].bitcast(I32), 0)
+        nc.vector.memset(bias_rows[:], 0.0)
+        nc.vector.memset(w2_planes[:].bitcast(I32), 0)
+        nc.vector.memset(wv_planes[:].bitcast(I32), 0)
+
+        def load_planes(planes, scales):
+            rows = PACK * scales.shape[0]
+            for quadrant in range(QUADRANTS):
+                nc.sync.dma_start(
+                    out=planes[32 * quadrant : 32 * quadrant + rows, :].bitcast(I32),
+                    in_=scales[:, 4 * quadrant : 4 * quadrant + 4, :].bitcast(I32),
+                )
+
+        def load_words(words, first, width, name):
+            loaded = keep.tile([P, words.shape[0], width], I32, name=name, align_bytes=64)
+            nc.sync.dma_start(
+                out=loaded[:],
+                in_=words.rearrange("g p n t -> p g (n t)").bitcast(I32)[:, :, first : first + width],
+            )
+            return loaded
+
+        def load_x(c):
+            loaded = []
+            for s in range(TOKEN_TILES):
+                x_tile = keep.tile([P, D_MODEL], BF16, name="x_%d_%d" % (c, s))
+                first = CHUNK * c + P * s
+                nc.sync.dma_start(out=x_tile[:], in_=x_rows[first : first + P, :])
+                loaded.append(x_tile)
+            return loaded
+
+        identity = keep.tile([P, P], F32)
+        make_identity(nc, identity[:])
+        nc.gpsimd.dma_start(out=bias_rows[B1_COL:B2G_COL, :], in_=b1.rearrange("(j m) -> j m", m=P))
+        nc.gpsimd.dma_start(out=bias_rows[B2G_COL:BV_COL, :], in_=b2g.rearrange("(j m) -> j m", m=P))
+        nc.gpsimd.dma_start(
+            out=bias_rows[BV_COL : BV_COL + OUT_TILES, :], in_=bv.rearrange("(j m) -> j m", m=P)
+        )
+
+        load_planes(w1_planes, W1_scales)
+        x_tiles = {0: load_x(0)}
+        w1_words = [load_words(W1_words, K_PASS * unit, K_PASS, "w1_%d" % unit) for unit in range(H_PASSES)]
+        x_tiles[1] = load_x(1)
+        load_planes(w2_planes, W2g_scales)
+        load_planes(wv_planes, Wv_scales)
+        half_width = BLOCK * P
+        w2_words = [load_words(W2g_words, 0, half_width, "w2_0")]
+        wv_words = [load_words(Wv_words, 0, half_width, "wv_0")]
+
+        xq_words, xq_scales = {}, {}
+
+        def quantise_x(c):
+            for g in range(X_PASSES):
+                xq_words[c, g] = keep.tile([P, CHUNK], I32, name="xq_words_%d_%d" % (c, g), align_bytes=64)
+                xq_scales[c, g] = keep.tile([P, CHUNK], U8, name="xq_scales_%d_%d" % (c, g), align_bytes=64)
+            for pair in range(TOKEN_TILES // 2):
+                banks = [
+                    flipped.tile([P, 2, 2 * P], F32, name="x_bank_%d" % g, tag="flipped")
+                    for g in range(X_PASSES)
+                ]
+                for s in range(2):
+                    x_as_words = x_tiles[c][2 * pair + s][:].bitcast(F32)
+                    for g in range(X_PASSES):
+                        for u in range(2):
+                            nc.tensor.transpose(
+                                out=banks[g][:, u, P * s : P * (s + 1)],
+                                in_=x_as_words[:, 2 * P * g + u : 2 * P * (g + 1) : 2],
+                                identity=identity[:],
+                            )
+                grouped = []
+                for g in range(X_PASSES):
+                    x_grouped = stage.tile([P, 2 * P, PACK], BF16, name="x_grouped_%d" % g, align_bytes=64)
+                    nc.vector.tensor_copy(
+                        out=x_grouped[:].rearrange("p w t -> p (w t)").bitcast(F32).rearrange("p (w u) -> p w u", u=2),
+                        in_=banks[g][:].rearrange("p u w -> p w u"),
+                    )
+                    grouped.append(x_grouped)
+                for g in range(X_PASSES):
+                    tokens = slice(2 * P * pair, 2 * P * (pair + 1))
+                    nc.vector.quantize_mx(
+                        out=xq_words[c, g][:, tokens].bitcast(FP8X4),
+                        scales=xq_scales[c, g][:, tokens],
+                        in_=grouped[g][:].rearrange("p w t -> p (w t)"),
+                    )
+
+        h_rows = {}
+
+        def hidden(c):
+            for unit in range(H_PASSES):
+                h_cols = stage.tile([P, UNIT_TILES, CHUNK], BF16)
+                for j in range(UNIT_TILES):
+                    features = slice(P * j, P * (j + 1))
+                    tile_index = UNIT_TILES * unit + j
+                    z = sums.tile([P, CHUNK], F32, tag="sums")
+                    for g in range(X_PASSES):
+                        nc.tensor.matmul_mx(
+                            out=z[:],
+                            lhsT=w1_words[unit][:, g, features].bitcast(FP8X4),
+                            lhsT_scale=w1_planes[PACK * g : P, P * tile_index : P * (tile_index + 1)],
+                            rhs=xq_words[c, g][:].bitcast(FP8X4),
+                            rhs_scale=xq_scales[c, g][:],
+                            start=(g == 0),
+                            stop=(g == X_PASSES - 1),
+                        )
+                    nc.scalar.activation(
+                        out=h_cols[:, j, :],
+                        in_=z[:],
+                        func=ACT.Silu,
+                        bias=bias_cols[:, B1_COL + tile_index : B1_COL + tile_index + 1],
+                        scale=1.0,
+                    )
+                parked = park_rows[CHUNK * c + P * unit : CHUNK * c + P * (unit + 1), :]
+                nc.sync.dma_start(
+                    out=parked.rearrange("(j a) (t w) -> (a t) j w", j=UNIT_TILES, t=PACK), in_=h_cols[:]
+                )
+            for unit in range(H_PASSES):
+                h_rows[c, unit] = stage.tile([P, PACK, CHUNK], BF16, name="h_rows")
+                nc.sync.dma_start(
+                    out=h_rows[c, unit][:].rearrange("p t w -> p (t w)"),
+                    in_=park_rows[CHUNK * c + P * unit : CHUNK * c + P * (unit + 1), :],
+                )
+
+        hq_words, hq_scales = {}, {}
+
+        def quantise_h(c, unit):
+            hq_words[c, unit] = keep.tile([P, CHUNK], I32, name="hq_words_%d_%d" % (c, unit), align_bytes=64)
+            hq_scales[c, unit] = keep.tile([P, CHUNK], U8, name="hq_scales_%d_%d" % (c, unit), align_bytes=64)
+            h_grouped = stage.tile([P, CHUNK, PACK], BF16, align_bytes=64)
+            nc.vector.tensor_copy(
+                out=h_grouped[:].rearrange("p (c i) t -> p c t i", i=4),
+                in_=h_rows[c, unit][:].rearrange("p t (c i) -> p c t i", i=4),
+            )
+            nc.vector.quantize_mx(
+                out=hq_words[c, unit][:].bitcast(FP8X4),
+                scales=hq_scales[c, unit][:],
+                in_=h_grouped[:].rearrange("p w t -> p (w t)"),
+            )
+
+        def mix(c, i):
+            half, features = i // BLOCK, slice(P * (i % BLOCK), P * (i % BLOCK + 1))
+            gate = sums.tile([P, CHUNK], F32, tag="sums")
+            for g in range(H_PASSES):
+                nc.tensor.matmul_mx(
+                    out=gate[:],
+                    lhsT=w2_words[half][:, g, features].bitcast(FP8X4),
+                    lhsT_scale=w2_planes[PACK * g : P, P * i : P * (i + 1)],
+                    rhs=hq_words[c, g][:].bitcast(FP8X4),
+                    rhs_scale=hq_scales[c, g][:],
+                    start=(g == 0),
+                    stop=(g == H_PASSES - 1),
+                )
+            value = sums.tile([P, CHUNK], F32, tag="sums")
+            for g in range(X_PASSES):
+                nc.tensor.matmul_mx(
+                    out=value[:],
+                    lhsT=wv_words[half][:, g, features].bitcast(FP8X4),
+                    lhsT_scale=wv_planes[PACK * g : P, P * i : P * (i + 1)],
+                    rhs=xq_words[c, g][:].bitcast(FP8X4),
+                    rhs_scale=xq_scales[c, g][:],
+                    start=(g == 0),
+                    stop=(g == X_PASSES - 1),
+                )
+            opened = mixing.tile([P, CHUNK], F32)
+            nc.scalar.activation(
+                out=opened[:], in_=gate[:], func=ACT.Sigmoid, bias=bias_cols[:, B2G_COL + i : B2G_COL + i + 1], scale=1.0
+            )
+            mixed = mixing.tile([P, CHUNK], F32)
+            nc.vector.scalar_tensor_tensor(
+                out=mixed[:],
+                in0=value[:],
+                scalar=bias_cols[:, BV_COL + i : BV_COL + i + 1],
+                in1=opened[:],
+                op0=ALU.add,
+                op1=ALU.mult,
+            )
+            return mixed
+
+        def store_block(c, half, block):
+            banks = [flipped.tile([P, BLOCK * P], F32, name="out_bank_%d" % s, tag="flipped") for s in range(TOKEN_TILES)]
+            for i in range(BLOCK):
+                for s in range(TOKEN_TILES):
+                    nc.tensor.transpose(
+                        out=banks[s][:, P * i : P * (i + 1)], in_=block[i][:, P * s : P * (s + 1)], identity=identity[:]
+                    )
+            for s in range(TOKEN_TILES):
+                result = results.tile([P, BLOCK * P], F32)
+                if s % 2 == 0:
+                    nc.scalar.copy(out=result[:], in_=banks[s][:])
+                else:
+                    nc.vector.tensor_copy(out=result[:], in_=banks[s][:])
+                first = CHUNK * c + P * s
+                nc.sync.dma_start(
+                    out=out_rows[first : first + P, BLOCK * P * half : BLOCK * P * (half + 1)], in_=result[:]
+                )
+
+        quantise_x(0)
+
+        bias_rows_f32 = keep.tile([P, P], F32)
+        nc.vector.tensor_copy(out=bias_rows_f32[:], in_=bias_rows[:])
+        bias_bank = flipped.tile([P, P], F32, tag="flipped")
+        nc.tensor.transpose(out=bias_bank[:], in_=bias_rows_f32[:], identity=identity[:])
+        bias_cols = keep.tile([P, P], F32)
+        nc.vector.tensor_copy(out=bias_cols[:], in_=bias_bank[:])
+
+        hidden(0)
+        w2_words.append(load_words(W2g_words, half_width, half_width, "w2_1"))
+        wv_words.append(load_words(Wv_words, half_width, half_width, "wv_1"))
+        quantise_x(1)
+        for unit in range(H_PASSES):
+            quantise_h(0, unit)
+        hidden(1)
+
+        block = []
+        for n in range(N_CHUNKS * OUT_TILES):
+            c, i = divmod(n, OUT_TILES)
+            block.append(mix(c, i))
+            if len(block) == BLOCK + 1:
+                done = n // BLOCK - 1
+                store_block(done // BLOCKS, done % BLOCKS, block[:BLOCK])
+                block = block[BLOCK:]
+            if c + 1 < N_CHUNKS and i % 2 == 0 and 0 < i // 2 <= H_PASSES:
+                quantise_h(c + 1, i // 2 - 1)
+        store_block(N_CHUNKS - 1, BLOCKS - 1, block)

@@ -14,22 +14,24 @@ ALU = mybir.AluOpType
 P = 128
 PACK = 4
 K_PASS = P * PACK
+BANK = 512
 TOKENS = 1024
 D_MODEL = 1024
 D_HIDDEN = 1536
-CHUNK = 512
+CHUNK = BANK
 N_CHUNKS = TOKENS // CHUNK
 TOKEN_TILES = CHUNK // P
 X_PASSES = D_MODEL // K_PASS
 H_PASSES = D_HIDDEN // K_PASS
 UNIT_TILES = K_PASS // P
-OUT_TILES = D_MODEL // P
-BLOCK = CHUNK // P
+GATE_TILES = D_MODEL // P
+HALVES = D_MODEL // BANK
+BLOCK = BANK // P
+LAG = 2
+ROUND_TRIP = 2
 QUADRANTS = 4
-BLOCKS = OUT_TILES // BLOCK
 B1_COL = 0
 B2G_COL = B1_COL + D_HIDDEN // P
-BV_COL = B2G_COL + OUT_TILES
 
 FLOPS = 2 * TOKENS * (D_MODEL * D_HIDDEN + D_HIDDEN * D_MODEL + D_MODEL * D_MODEL)
 
@@ -46,7 +48,7 @@ def tile_selectivemixing_pa_kernel(
         ctx.enter_context(tc.manual_schedule())
         keep = ctx.enter_context(tc.tile_pool(name="keep", bufs=1))
         stage = ctx.enter_context(tc.tile_pool(name="stage", bufs=3))
-        mixing = ctx.enter_context(tc.tile_pool(name="mixing", bufs=BLOCK + 2))
+        gates = ctx.enter_context(tc.tile_pool(name="gates", bufs=BLOCK + LAG + 1))
         results = ctx.enter_context(tc.tile_pool(name="results", bufs=2 * TOKEN_TILES))
         sums = ctx.enter_context(tc.psum_pool(name="sums", bufs=4))
         flipped = ctx.enter_context(tc.psum_pool(name="flipped", bufs=4))
@@ -55,10 +57,16 @@ def tile_selectivemixing_pa_kernel(
         w2_planes = keep.tile([P, D_MODEL], U8, align_bytes=64)
         wv_planes = keep.tile([P, D_MODEL], U8, align_bytes=64)
         bias_rows = keep.tile([P, P], BF16)
-        nc.vector.memset(w1_planes[:].bitcast(I32), 0)
+        bv_row = keep.tile([P, D_MODEL], BF16)
+        ones = keep.tile([P, P], BF16)
         nc.vector.memset(bias_rows[:], 0.0)
-        nc.vector.memset(w2_planes[:].bitcast(I32), 0)
+        nc.vector.memset(bv_row[:], 0.0)
+        nc.vector.memset(ones[:], 1.0)
+        nc.vector.memset(w1_planes[:].bitcast(I32), 0)
         nc.vector.memset(wv_planes[:].bitcast(I32), 0)
+        nc.vector.memset(w2_planes[:].bitcast(I32), 0)
+        identity = keep.tile([P, P], F32)
+        make_identity(nc, identity[:])
 
         def load_planes(planes, scales):
             rows = PACK * scales.shape[0]
@@ -68,11 +76,11 @@ def tile_selectivemixing_pa_kernel(
                     in_=scales[:, 4 * quadrant : 4 * quadrant + 4, :].bitcast(I32),
                 )
 
-        def load_words(words, first, width, name):
-            loaded = keep.tile([P, words.shape[0], width], I32, name=name, align_bytes=64)
+        def load_words(words, piece, name):
+            loaded = keep.tile([P, words.shape[0], BANK], I32, name="%s_%d" % (name, piece), align_bytes=64)
             nc.sync.dma_start(
                 out=loaded[:],
-                in_=words.rearrange("g p n t -> p g (n t)").bitcast(I32)[:, :, first : first + width],
+                in_=words.rearrange("g p n t -> p g (n t)").bitcast(I32)[:, :, BANK * piece : BANK * (piece + 1)],
             )
             return loaded
 
@@ -85,23 +93,20 @@ def tile_selectivemixing_pa_kernel(
                 loaded.append(x_tile)
             return loaded
 
-        identity = keep.tile([P, P], F32)
-        make_identity(nc, identity[:])
-        nc.gpsimd.dma_start(out=bias_rows[B1_COL:B2G_COL, :], in_=b1.rearrange("(j m) -> j m", m=P))
-        nc.gpsimd.dma_start(out=bias_rows[B2G_COL:BV_COL, :], in_=b2g.rearrange("(j m) -> j m", m=P))
-        nc.gpsimd.dma_start(
-            out=bias_rows[BV_COL : BV_COL + OUT_TILES, :], in_=bv.rearrange("(j m) -> j m", m=P)
-        )
-
+        nc.scalar.dma_start(out=bias_rows[B1_COL:B2G_COL, :], in_=b1.rearrange("(j m) -> j m", m=P))
+        nc.scalar.dma_start(out=bias_rows[B2G_COL : B2G_COL + GATE_TILES, :], in_=b2g.rearrange("(j m) -> j m", m=P))
+        nc.scalar.dma_start(out=bv_row[0:1, :], in_=bv.rearrange("(o d) -> o d", o=1))
+        warm = keep.tile([P, 1], F32)
+        nc.scalar.activation(out=warm[:], in_=ones[:, 0:1], func=ACT.Silu)
+        x_tiles = [load_x(0)]
         load_planes(w1_planes, W1_scales)
-        x_tiles = {0: load_x(0)}
-        w1_words = [load_words(W1_words, K_PASS * unit, K_PASS, "w1_%d" % unit) for unit in range(H_PASSES)]
-        x_tiles[1] = load_x(1)
-        load_planes(w2_planes, W2g_scales)
+        w1_words = [load_words(W1_words, 0, "w1")]
         load_planes(wv_planes, Wv_scales)
-        half_width = BLOCK * P
-        w2_words = [load_words(W2g_words, 0, half_width, "w2_0")]
-        wv_words = [load_words(Wv_words, 0, half_width, "wv_0")]
+        wv_words = [load_words(Wv_words, 0, "wv")]
+        w1_words.append(load_words(W1_words, 1, "w1"))
+        x_tiles.append(load_x(1))
+        wv_words.append(load_words(Wv_words, 1, "wv"))
+        w1_words.append(load_words(W1_words, 2, "w1"))
 
         xq_words, xq_scales = {}, {}
 
@@ -111,8 +116,7 @@ def tile_selectivemixing_pa_kernel(
                 xq_scales[c, g] = keep.tile([P, CHUNK], U8, name="xq_scales_%d_%d" % (c, g), align_bytes=64)
             for pair in range(TOKEN_TILES // 2):
                 banks = [
-                    flipped.tile([P, 2, 2 * P], F32, name="x_bank_%d" % g, tag="flipped")
-                    for g in range(X_PASSES)
+                    flipped.tile([P, 2, 2 * P], F32, name="x_bank_%d" % g, tag="flipped") for g in range(X_PASSES)
                 ]
                 for s in range(2):
                     x_as_words = x_tiles[c][2 * pair + s][:].bitcast(F32)
@@ -123,14 +127,14 @@ def tile_selectivemixing_pa_kernel(
                                 in_=x_as_words[:, 2 * P * g + u : 2 * P * (g + 1) : 2],
                                 identity=identity[:],
                             )
-                grouped = []
-                for g in range(X_PASSES):
-                    x_grouped = stage.tile([P, 2 * P, PACK], BF16, name="x_grouped_%d" % g, align_bytes=64)
-                    nc.vector.tensor_copy(
-                        out=x_grouped[:].rearrange("p w t -> p (w t)").bitcast(F32).rearrange("p (w u) -> p w u", u=2),
-                        in_=banks[g][:].rearrange("p u w -> p w u"),
-                    )
-                    grouped.append(x_grouped)
+                grouped = [
+                    stage.tile([P, 2 * P, PACK], BF16, name="x_grouped_%d" % g, align_bytes=64) for g in range(X_PASSES)
+                ]
+                word_views = [
+                    t[:].rearrange("p w t -> p (w t)").bitcast(F32).rearrange("p (w u) -> p w u", u=2) for t in grouped
+                ]
+                nc.scalar.copy(out=word_views[0], in_=banks[0][:].rearrange("p u w -> p w u"))
+                nc.vector.tensor_copy(out=word_views[1], in_=banks[1][:].rearrange("p u w -> p w u"))
                 for g in range(X_PASSES):
                     tokens = slice(2 * P * pair, 2 * P * (pair + 1))
                     nc.vector.quantize_mx(
@@ -139,42 +143,59 @@ def tile_selectivemixing_pa_kernel(
                         in_=grouped[g][:].rearrange("p w t -> p (w t)"),
                     )
 
+        def hidden_tile(c, unit, j, h_cols):
+            tile_index = UNIT_TILES * unit + j
+            z = sums.tile([P, CHUNK], F32, tag="sums")
+            for g in range(X_PASSES):
+                nc.tensor.matmul_mx(
+                    out=z[:],
+                    lhsT=w1_words[unit][:, g, P * j : P * (j + 1)].bitcast(FP8X4),
+                    lhsT_scale=w1_planes[PACK * g : P, P * tile_index : P * (tile_index + 1)],
+                    rhs=xq_words[c, g][:].bitcast(FP8X4),
+                    rhs_scale=xq_scales[c, g][:],
+                    start=(g == 0),
+                    stop=(g == X_PASSES - 1),
+                )
+            nc.scalar.activation(
+                out=h_cols[:, j, :],
+                in_=z[:],
+                func=ACT.Silu,
+                bias=bias_cols[:, B1_COL + tile_index : B1_COL + tile_index + 1],
+                scale=1.0,
+            )
+
+        values = {}
+
+        def value_tile(c, half, s):
+            v = sums.tile([P, BANK], F32, tag="sums")
+            for g in range(X_PASSES):
+                nc.tensor.matmul_mx(
+                    out=v[:],
+                    lhsT=xq_words[c, g][:, P * s : P * (s + 1)].bitcast(FP8X4),
+                    lhsT_scale=xq_scales[c, g][:, P * s : P * (s + 1)],
+                    rhs=wv_words[half][:, g, :].bitcast(FP8X4),
+                    rhs_scale=wv_planes[PACK * g : P, BANK * half : BANK * (half + 1)],
+                    start=(g == 0),
+                    stop=(g == X_PASSES - 1),
+                )
+            values[c, half, s] = keep.tile([P, BANK], F32, name="value_%d_%d_%d" % (c, half, s))
+            nc.vector.tensor_tensor(
+                out=values[c, half, s][:], in0=v[:], in1=bv_all[:, BANK * half : BANK * (half + 1)], op=ALU.add
+            )
+
+        def parking_place(c, unit):
+            return park_rows[CHUNK * c + P * unit : CHUNK * c + P * (unit + 1), :]
+
+        def park(c, unit, h_cols):
+            nc.sync.dma_start(
+                out=parking_place(c, unit).rearrange("(j a) (t w) -> (a t) j w", j=UNIT_TILES, t=PACK), in_=h_cols[:]
+            )
+
         h_rows = {}
 
-        def hidden(c):
-            for unit in range(H_PASSES):
-                h_cols = stage.tile([P, UNIT_TILES, CHUNK], BF16)
-                for j in range(UNIT_TILES):
-                    features = slice(P * j, P * (j + 1))
-                    tile_index = UNIT_TILES * unit + j
-                    z = sums.tile([P, CHUNK], F32, tag="sums")
-                    for g in range(X_PASSES):
-                        nc.tensor.matmul_mx(
-                            out=z[:],
-                            lhsT=w1_words[unit][:, g, features].bitcast(FP8X4),
-                            lhsT_scale=w1_planes[PACK * g : P, P * tile_index : P * (tile_index + 1)],
-                            rhs=xq_words[c, g][:].bitcast(FP8X4),
-                            rhs_scale=xq_scales[c, g][:],
-                            start=(g == 0),
-                            stop=(g == X_PASSES - 1),
-                        )
-                    nc.scalar.activation(
-                        out=h_cols[:, j, :],
-                        in_=z[:],
-                        func=ACT.Silu,
-                        bias=bias_cols[:, B1_COL + tile_index : B1_COL + tile_index + 1],
-                        scale=1.0,
-                    )
-                parked = park_rows[CHUNK * c + P * unit : CHUNK * c + P * (unit + 1), :]
-                nc.sync.dma_start(
-                    out=parked.rearrange("(j a) (t w) -> (a t) j w", j=UNIT_TILES, t=PACK), in_=h_cols[:]
-                )
-            for unit in range(H_PASSES):
-                h_rows[c, unit] = stage.tile([P, PACK, CHUNK], BF16, name="h_rows")
-                nc.sync.dma_start(
-                    out=h_rows[c, unit][:].rearrange("p t w -> p (t w)"),
-                    in_=park_rows[CHUNK * c + P * unit : CHUNK * c + P * (unit + 1), :],
-                )
+        def fetch(c, unit):
+            h_rows[c, unit] = stage.tile([P, PACK, CHUNK], BF16, name="h_rows")
+            nc.sync.dma_start(out=h_rows[c, unit][:].rearrange("p t w -> p (t w)"), in_=parking_place(c, unit))
 
         hq_words, hq_scales = {}, {}
 
@@ -192,88 +213,89 @@ def tile_selectivemixing_pa_kernel(
                 in_=h_grouped[:].rearrange("p w t -> p (w t)"),
             )
 
-        def mix(c, i):
-            half, features = i // BLOCK, slice(P * (i % BLOCK), P * (i % BLOCK + 1))
-            gate = sums.tile([P, CHUNK], F32, tag="sums")
+        def gate_tile(c, i):
+            half, j = divmod(i, BLOCK)
+            y = sums.tile([P, CHUNK], F32, tag="sums")
             for g in range(H_PASSES):
                 nc.tensor.matmul_mx(
-                    out=gate[:],
-                    lhsT=w2_words[half][:, g, features].bitcast(FP8X4),
+                    out=y[:],
+                    lhsT=w2_words[half][:, g, P * j : P * (j + 1)].bitcast(FP8X4),
                     lhsT_scale=w2_planes[PACK * g : P, P * i : P * (i + 1)],
                     rhs=hq_words[c, g][:].bitcast(FP8X4),
                     rhs_scale=hq_scales[c, g][:],
                     start=(g == 0),
                     stop=(g == H_PASSES - 1),
                 )
-            value = sums.tile([P, CHUNK], F32, tag="sums")
-            for g in range(X_PASSES):
-                nc.tensor.matmul_mx(
-                    out=value[:],
-                    lhsT=wv_words[half][:, g, features].bitcast(FP8X4),
-                    lhsT_scale=wv_planes[PACK * g : P, P * i : P * (i + 1)],
-                    rhs=xq_words[c, g][:].bitcast(FP8X4),
-                    rhs_scale=xq_scales[c, g][:],
-                    start=(g == 0),
-                    stop=(g == X_PASSES - 1),
-                )
-            opened = mixing.tile([P, CHUNK], F32)
+            gate = gates.tile([P, CHUNK], F32)
             nc.scalar.activation(
-                out=opened[:], in_=gate[:], func=ACT.Sigmoid, bias=bias_cols[:, B2G_COL + i : B2G_COL + i + 1], scale=1.0
+                out=gate[:], in_=y[:], func=ACT.Sigmoid, bias=bias_cols[:, B2G_COL + i : B2G_COL + i + 1], scale=1.0
             )
-            mixed = mixing.tile([P, CHUNK], F32)
-            nc.vector.scalar_tensor_tensor(
-                out=mixed[:],
-                in0=value[:],
-                scalar=bias_cols[:, BV_COL + i : BV_COL + i + 1],
-                in1=opened[:],
-                op0=ALU.add,
-                op1=ALU.mult,
-            )
-            return mixed
+            return gate
 
-        def store_block(c, half, block):
-            banks = [flipped.tile([P, BLOCK * P], F32, name="out_bank_%d" % s, tag="flipped") for s in range(TOKEN_TILES)]
-            for i in range(BLOCK):
+        def finish_block(c, half, block):
+            banks = [flipped.tile([P, BANK], F32, name="gate_bank_%d" % s, tag="flipped") for s in range(TOKEN_TILES)]
+            for j in range(BLOCK):
                 for s in range(TOKEN_TILES):
                     nc.tensor.transpose(
-                        out=banks[s][:, P * i : P * (i + 1)], in_=block[i][:, P * s : P * (s + 1)], identity=identity[:]
+                        out=banks[s][:, P * j : P * (j + 1)], in_=block[j][:, P * s : P * (s + 1)], identity=identity[:]
                     )
             for s in range(TOKEN_TILES):
-                result = results.tile([P, BLOCK * P], F32)
-                if s % 2 == 0:
-                    nc.scalar.copy(out=result[:], in_=banks[s][:])
-                else:
-                    nc.vector.tensor_copy(out=result[:], in_=banks[s][:])
+                result = results.tile([P, BANK], F32)
+                nc.vector.tensor_tensor(out=result[:], in0=banks[s][:], in1=values[c, half, s][:], op=ALU.mult)
                 first = CHUNK * c + P * s
-                nc.sync.dma_start(
-                    out=out_rows[first : first + P, BLOCK * P * half : BLOCK * P * (half + 1)], in_=result[:]
-                )
-
-        quantise_x(0)
+                nc.sync.dma_start(out=out_rows[first : first + P, BANK * half : BANK * (half + 1)], in_=result[:])
 
         bias_rows_f32 = keep.tile([P, P], F32)
         nc.vector.tensor_copy(out=bias_rows_f32[:], in_=bias_rows[:])
+
+        quantise_x(0)
+
         bias_bank = flipped.tile([P, P], F32, tag="flipped")
         nc.tensor.transpose(out=bias_bank[:], in_=bias_rows_f32[:], identity=identity[:])
         bias_cols = keep.tile([P, P], F32)
         nc.vector.tensor_copy(out=bias_cols[:], in_=bias_bank[:])
+        bv_all = keep.tile([P, D_MODEL], F32)
+        for half in range(HALVES):
+            bv_bank = flipped.tile([P, BANK], F32, tag="flipped")
+            nc.tensor.matmul(
+                out=bv_bank[:], lhsT=ones[:], rhs=bv_row[:, BANK * half : BANK * (half + 1)], start=True, stop=True
+            )
+            nc.scalar.copy(out=bv_all[:, BANK * half : BANK * (half + 1)], in_=bv_bank[:])
 
-        hidden(0)
-        w2_words.append(load_words(W2g_words, half_width, half_width, "w2_1"))
-        wv_words.append(load_words(Wv_words, half_width, half_width, "wv_1"))
-        quantise_x(1)
-        for unit in range(H_PASSES):
-            quantise_h(0, unit)
-        hidden(1)
+        w2_words = []
+        parked = []
+        for c in range(N_CHUNKS):
+            for unit in range(H_PASSES):
+                if unit == H_PASSES - 1 and c + 1 < N_CHUNKS:
+                    quantise_x(c + 1)
+                h_cols = stage.tile([P, UNIT_TILES, CHUNK], BF16)
+                for j in range(UNIT_TILES):
+                    hidden_tile(c, unit, j, h_cols)
+                    trio, place = divmod(UNIT_TILES * unit + j, 3)
+                    if place > 0:
+                        half, s = divmod(2 * trio + place - 1, TOKEN_TILES)
+                        value_tile(c, half, s)
+                park(c, unit, h_cols)
+                if parked:
+                    fetch(*parked[-1])
+                parked.append((c, unit))
+                if len(parked) > ROUND_TRIP:
+                    quantise_h(*parked[0])
+                    parked = parked[1:]
+                if not w2_words:
+                    load_planes(w2_planes, W2g_scales)
+                    w2_words.extend(load_words(W2g_words, half, "w2") for half in range(HALVES))
+        fetch(*parked[-1])
 
         block = []
-        for n in range(N_CHUNKS * OUT_TILES):
-            c, i = divmod(n, OUT_TILES)
-            block.append(mix(c, i))
-            if len(block) == BLOCK + 1:
-                done = n // BLOCK - 1
-                store_block(done // BLOCKS, done % BLOCKS, block[:BLOCK])
+        for n in range(N_CHUNKS * GATE_TILES):
+            c, i = divmod(n, GATE_TILES)
+            block.append(gate_tile(c, i))
+            if len(block) == BLOCK + LAG:
+                for late in parked:
+                    quantise_h(*late)
+                parked = []
+                done = (n - LAG) // BLOCK
+                finish_block(done // HALVES, done % HALVES, block[:BLOCK])
                 block = block[BLOCK:]
-            if c + 1 < N_CHUNKS and i % 2 == 0 and 0 < i // 2 <= H_PASSES:
-                quantise_h(c + 1, i // 2 - 1)
-        store_block(N_CHUNKS - 1, BLOCKS - 1, block)
+        finish_block(N_CHUNKS - 1, HALVES - 1, block)

@@ -27,6 +27,9 @@ UNIT_TILES = K_PASS // P
 GATE_TILES = D_MODEL // P
 HALVES = D_MODEL // BANK
 BLOCK = BANK // P
+HIDDEN_TILES = D_HIDDEN // P
+VALUE_TILES = HALVES * TOKEN_TILES
+H_PER_VALUE = 3
 LAG = 2
 ROUND_TRIP = 2
 QUADRANTS = 4
@@ -266,26 +269,27 @@ def tile_selectivemixing_pa_kernel(
         parked = []
         for c in range(N_CHUNKS):
             for unit in range(H_PASSES):
+                if len(parked) > ROUND_TRIP:
+                    quantise_h(*parked[0])
+                    parked = parked[1:]
                 if unit == H_PASSES - 1 and c + 1 < N_CHUNKS:
                     quantise_x(c + 1)
                 h_cols = stage.tile([P, UNIT_TILES, CHUNK], BF16)
                 for j in range(UNIT_TILES):
                     hidden_tile(c, unit, j, h_cols)
-                    trio, place = divmod(UNIT_TILES * unit + j, 3)
-                    if place > 0:
-                        half, s = divmod(2 * trio + place - 1, TOKEN_TILES)
-                        value_tile(c, half, s)
+                    v, place = divmod(UNIT_TILES * unit + j, H_PER_VALUE)
+                    if place == H_PER_VALUE - 1:
+                        value_tile(c, v // TOKEN_TILES, v % TOKEN_TILES)
                 park(c, unit, h_cols)
-                if parked:
-                    fetch(*parked[-1])
+                if unit > 0:
+                    fetch(c, unit - 1)
                 parked.append((c, unit))
-                if len(parked) > ROUND_TRIP:
-                    quantise_h(*parked[0])
-                    parked = parked[1:]
                 if not w2_words:
                     load_planes(w2_planes, W2g_scales)
                     w2_words.extend(load_words(W2g_words, half, "w2") for half in range(HALVES))
-        fetch(*parked[-1])
+            for v in range(HIDDEN_TILES // H_PER_VALUE, VALUE_TILES):
+                value_tile(c, v // TOKEN_TILES, v % TOKEN_TILES)
+            fetch(c, H_PASSES - 1)
 
         block = []
         for n in range(N_CHUNKS * GATE_TILES):

@@ -22,19 +22,12 @@ CHUNK = BANK
 N_CHUNKS = TOKENS // CHUNK
 TOKEN_TILES = CHUNK // P
 X_PASSES = D_MODEL // K_PASS
-H_PASSES = D_HIDDEN // K_PASS
-UNIT_TILES = K_PASS // P
-GATE_TILES = D_MODEL // P
+UNITS = D_HIDDEN // K_PASS
 HALVES = D_MODEL // BANK
-BLOCK = BANK // P
-HIDDEN_TILES = D_HIDDEN // P
-VALUE_TILES = HALVES * TOKEN_TILES
-H_PER_VALUE = 3
-LAG = 2
-ROUND_TRIP = 2
 QUADRANTS = 4
-B1_COL = 0
-B2G_COL = B1_COL + D_HIDDEN // P
+SCALAR_GROUPS = ((0, 1), (1, 2))
+WARM_UP = 4
+RUN = 4
 
 FLOPS = 2 * TOKENS * (D_MODEL * D_HIDDEN + D_HIDDEN * D_MODEL + D_MODEL * D_MODEL)
 
@@ -45,28 +38,24 @@ def tile_selectivemixing_pa_kernel(
     nc = tc.nc
     x_rows = x.rearrange("b l d -> (b l) d")
     out_rows = out.rearrange("b l d -> (b l) d")
-    park_rows = out_rows.bitcast(BF16)
 
     with ExitStack() as ctx:
         ctx.enter_context(tc.manual_schedule())
         keep = ctx.enter_context(tc.tile_pool(name="keep", bufs=1))
-        stage = ctx.enter_context(tc.tile_pool(name="stage", bufs=3))
-        gates = ctx.enter_context(tc.tile_pool(name="gates", bufs=BLOCK + LAG + 1))
-        results = ctx.enter_context(tc.tile_pool(name="results", bufs=2 * TOKEN_TILES))
-        sums = ctx.enter_context(tc.psum_pool(name="sums", bufs=4))
-        flipped = ctx.enter_context(tc.psum_pool(name="flipped", bufs=4))
+        stage = ctx.enter_context(tc.tile_pool(name="stage", bufs=4))
+        results = ctx.enter_context(tc.tile_pool(name="results", bufs=6))
+        sums = ctx.enter_context(tc.psum_pool(name="sums", bufs=6))
+        flipped = ctx.enter_context(tc.psum_pool(name="flipped", bufs=2))
 
+        wv_planes = keep.tile([P, D_MODEL], U8, align_bytes=64)
         w1_planes = keep.tile([P, D_HIDDEN], U8, align_bytes=64)
         w2_planes = keep.tile([P, D_MODEL], U8, align_bytes=64)
-        wv_planes = keep.tile([P, D_MODEL], U8, align_bytes=64)
-        bias_rows = keep.tile([P, P], BF16)
         bv_row = keep.tile([P, D_MODEL], BF16)
-        ones = keep.tile([P, P], BF16)
-        nc.vector.memset(bias_rows[:], 0.0)
-        nc.vector.memset(bv_row[:], 0.0)
+        ones = keep.tile([P, BANK], BF16)
         nc.vector.memset(ones[:], 1.0)
-        nc.vector.memset(w1_planes[:].bitcast(I32), 0)
+        nc.vector.memset(bv_row[:].bitcast(I32), 0)
         nc.vector.memset(wv_planes[:].bitcast(I32), 0)
+        nc.vector.memset(w1_planes[:].bitcast(I32), 0)
         nc.vector.memset(w2_planes[:].bitcast(I32), 0)
         identity = keep.tile([P, P], F32)
         make_identity(nc, identity[:])
@@ -87,84 +76,107 @@ def tile_selectivemixing_pa_kernel(
             )
             return loaded
 
-        def load_x(c):
-            loaded = []
-            for s in range(TOKEN_TILES):
-                x_tile = keep.tile([P, D_MODEL], BF16, name="x_%d_%d" % (c, s))
-                first = CHUNK * c + P * s
-                nc.sync.dma_start(out=x_tile[:], in_=x_rows[first : first + P, :])
-                loaded.append(x_tile)
-            return loaded
+        x_tiles = {}
 
-        nc.scalar.dma_start(out=bias_rows[B1_COL:B2G_COL, :], in_=b1.rearrange("(j m) -> j m", m=P))
-        nc.scalar.dma_start(out=bias_rows[B2G_COL : B2G_COL + GATE_TILES, :], in_=b2g.rearrange("(j m) -> j m", m=P))
+        def load_x(c, s, count):
+            loaded = keep.tile([P, count, D_MODEL], BF16, name="x_%d_%d" % (c, s))
+            first = CHUNK * c + P * s
+            nc.sync.dma_start(
+                out=loaded[:], in_=x_rows[first : first + P * count, :].rearrange("(s p) d -> p s d", p=P)
+            )
+            for i in range(count):
+                x_tiles[c, s + i] = loaded[:, i, :]
+
+        b1_cols = keep.tile([P, UNITS * PACK], BF16)
         nc.scalar.dma_start(out=bv_row[0:1, :], in_=bv.rearrange("(o d) -> o d", o=1))
         warm = keep.tile([P, 1], F32)
         nc.scalar.activation(out=warm[:], in_=ones[:, 0:1], func=ACT.Silu)
-        x_tiles = [load_x(0)]
-        load_planes(w1_planes, W1_scales)
-        w1_words = [load_words(W1_words, 0, "w1")]
+        load_x(0, 0, 1)
+        load_x(0, 1, 1)
         load_planes(wv_planes, Wv_scales)
         wv_words = [load_words(Wv_words, 0, "wv")]
-        w1_words.append(load_words(W1_words, 1, "w1"))
-        x_tiles.append(load_x(1))
+        load_x(0, 2, 2)
         wv_words.append(load_words(Wv_words, 1, "wv"))
-        w1_words.append(load_words(W1_words, 2, "w1"))
+        load_planes(w1_planes, W1_scales)
+        w1_words = [load_words(W1_words, 0, "w1")]
+        nc.sync.dma_start(
+            out=b1_cols[:].rearrange("p (u t) -> p u t", t=PACK), in_=b1.rearrange("(u p t) -> p u t", p=P, t=PACK)
+        )
+        load_x(1, 0, 2)
+        load_x(1, 2, 2)
+        w1_words.extend(load_words(W1_words, unit, "w1") for unit in range(1, UNITS))
+        load_planes(w2_planes, W2g_scales)
+        w2_words = [load_words(W2g_words, half, "w2") for half in range(HALVES)]
+        b2g_all = keep.tile([P, D_MODEL], BF16)
+        nc.sync.dma_start(out=b2g_all[:], in_=b2g.partition_broadcast(P))
 
         xq_words, xq_scales = {}, {}
+        for c in range(N_CHUNKS):
+            xq_words[c] = keep.tile([P, X_PASSES, CHUNK], I32, name="xq_words_%d" % c, align_bytes=64)
+            xq_scales[c] = keep.tile([P, X_PASSES, CHUNK], U8, name="xq_scales_%d" % c, align_bytes=64)
 
-        def quantise_x(c):
+        def transpose_x(c, s):
+            x_as_words = x_tiles[c, s].bitcast(F32)
+            bank = flipped.tile([P, X_PASSES, 2, P], F32, tag="flipped")
             for g in range(X_PASSES):
-                xq_words[c, g] = keep.tile([P, CHUNK], I32, name="xq_words_%d_%d" % (c, g), align_bytes=64)
-                xq_scales[c, g] = keep.tile([P, CHUNK], U8, name="xq_scales_%d_%d" % (c, g), align_bytes=64)
-            for pair in range(TOKEN_TILES // 2):
-                banks = [
-                    flipped.tile([P, 2, 2 * P], F32, name="x_bank_%d" % g, tag="flipped") for g in range(X_PASSES)
-                ]
-                for s in range(2):
-                    x_as_words = x_tiles[c][2 * pair + s][:].bitcast(F32)
-                    for g in range(X_PASSES):
-                        for u in range(2):
-                            nc.tensor.transpose(
-                                out=banks[g][:, u, P * s : P * (s + 1)],
-                                in_=x_as_words[:, 2 * P * g + u : 2 * P * (g + 1) : 2],
-                                identity=identity[:],
-                            )
-                grouped = [
-                    stage.tile([P, 2 * P, PACK], BF16, name="x_grouped_%d" % g, align_bytes=64) for g in range(X_PASSES)
-                ]
-                word_views = [
-                    t[:].rearrange("p w t -> p (w t)").bitcast(F32).rearrange("p (w u) -> p w u", u=2) for t in grouped
-                ]
-                nc.scalar.copy(out=word_views[0], in_=banks[0][:].rearrange("p u w -> p w u"))
-                nc.vector.tensor_copy(out=word_views[1], in_=banks[1][:].rearrange("p u w -> p w u"))
-                for g in range(X_PASSES):
-                    tokens = slice(2 * P * pair, 2 * P * (pair + 1))
-                    nc.vector.quantize_mx(
-                        out=xq_words[c, g][:, tokens].bitcast(FP8X4),
-                        scales=xq_scales[c, g][:, tokens],
-                        in_=grouped[g][:].rearrange("p w t -> p (w t)"),
+                for u in range(2):
+                    nc.tensor.transpose(
+                        out=bank[:, g, u, :],
+                        in_=x_as_words[:, 2 * P * g + u : 2 * P * (g + 1) : 2],
+                        identity=identity[:],
                     )
+            grouped = stage.tile([P, X_PASSES, P, PACK], BF16, name="x_grouped", align_bytes=64)
+            nc.scalar.copy(
+                out=grouped[:].rearrange("p g w t -> p (g w t)").bitcast(F32).rearrange("p (g w u) -> p g w u", g=X_PASSES, u=2),
+                in_=bank[:].rearrange("p g u w -> p g w u"),
+            )
+            return grouped
 
-        def hidden_tile(c, unit, j, h_cols):
-            tile_index = UNIT_TILES * unit + j
+        def quantise_x(c, s, grouped):
+            for g in range(X_PASSES):
+                nc.vector.quantize_mx(
+                    out=xq_words[c][:, g, P * s : P * (s + 1)].bitcast(FP8X4),
+                    scales=xq_scales[c][:, g, P * s : P * (s + 1)],
+                    in_=grouped[:, g].rearrange("p w t -> p (w t)"),
+                )
+
+        w1_sorted = [keep.tile([P, X_PASSES, K_PASS], I32, name="w1_sorted_%d" % u, align_bytes=64) for u in range(UNITS)]
+        w1_sorted_planes = keep.tile([P, D_HIDDEN], U8, align_bytes=64)
+
+        def sort_w1_planes(unit):
+            columns = slice(K_PASS * unit, K_PASS * (unit + 1))
+            nc.vector.tensor_copy(
+                out=w1_sorted_planes[:, columns].rearrange("p (t m) -> p m t", t=PACK),
+                in_=w1_planes[:, columns].rearrange("p (m t) -> p m t", t=PACK),
+            )
+
+        def sort_w1_words(unit):
+            for g in range(X_PASSES):
+                nc.vector.tensor_copy(
+                    out=w1_sorted[unit][:, g, :].rearrange("p (t c i) -> p c t i", t=PACK, i=RUN),
+                    in_=w1_words[unit][:, g, :].rearrange("p (c i t) -> p c t i", t=PACK, i=RUN),
+                )
+
+        h_cols = {}
+
+        def hidden_tile(c, unit, t):
+            if t == 0:
+                h_cols[c, unit] = stage.tile([P, PACK, CHUNK], BF16, name="h_cols")
             z = sums.tile([P, CHUNK], F32, tag="sums")
+            first = K_PASS * unit + P * t
             for g in range(X_PASSES):
                 nc.tensor.matmul_mx(
                     out=z[:],
-                    lhsT=w1_words[unit][:, g, P * j : P * (j + 1)].bitcast(FP8X4),
-                    lhsT_scale=w1_planes[PACK * g : P, P * tile_index : P * (tile_index + 1)],
-                    rhs=xq_words[c, g][:].bitcast(FP8X4),
-                    rhs_scale=xq_scales[c, g][:],
+                    lhsT=w1_sorted[unit][:, g, P * t : P * (t + 1)].bitcast(FP8X4),
+                    lhsT_scale=w1_sorted_planes[PACK * g : P, first : first + P],
+                    rhs=xq_words[c][:, g, :].bitcast(FP8X4),
+                    rhs_scale=xq_scales[c][:, g, :],
                     start=(g == 0),
                     stop=(g == X_PASSES - 1),
                 )
+            column = PACK * unit + t
             nc.scalar.activation(
-                out=h_cols[:, j, :],
-                in_=z[:],
-                func=ACT.Silu,
-                bias=bias_cols[:, B1_COL + tile_index : B1_COL + tile_index + 1],
-                scale=1.0,
+                out=h_cols[c, unit][:, t, :], in_=z[:], func=ACT.Silu, bias=b1_cols[:, column : column + 1], scale=1.0
             )
 
         values = {}
@@ -174,8 +186,8 @@ def tile_selectivemixing_pa_kernel(
             for g in range(X_PASSES):
                 nc.tensor.matmul_mx(
                     out=v[:],
-                    lhsT=xq_words[c, g][:, P * s : P * (s + 1)].bitcast(FP8X4),
-                    lhsT_scale=xq_scales[c, g][:, P * s : P * (s + 1)],
+                    lhsT=xq_words[c][:, g, P * s : P * (s + 1)].bitcast(FP8X4),
+                    lhsT_scale=xq_scales[c][:, g, P * s : P * (s + 1)],
                     rhs=wv_words[half][:, g, :].bitcast(FP8X4),
                     rhs_scale=wv_planes[PACK * g : P, BANK * half : BANK * (half + 1)],
                     start=(g == 0),
@@ -186,120 +198,141 @@ def tile_selectivemixing_pa_kernel(
                 out=values[c, half, s][:], in0=v[:], in1=bv_all[:, BANK * half : BANK * (half + 1)], op=ALU.add
             )
 
-        def parking_place(c, unit):
-            return park_rows[CHUNK * c + P * unit : CHUNK * c + P * (unit + 1), :]
+        hq_words, hq_scales, h_grouped = {}, {}, {}
 
-        def park(c, unit, h_cols):
-            nc.sync.dma_start(
-                out=parking_place(c, unit).rearrange("(j a) (t w) -> (a t) j w", j=UNIT_TILES, t=PACK), in_=h_cols[:]
+        def group_h(c, unit):
+            h_grouped[c, unit] = stage.tile([P, CHUNK, PACK], BF16, name="h_grouped", align_bytes=64)
+            copy = nc.scalar.copy if (c, unit) in SCALAR_GROUPS else nc.vector.tensor_copy
+            copy(
+                out=h_grouped[c, unit][:].rearrange("p (c i) t -> p c t i", i=RUN),
+                in_=h_cols[c, unit][:].rearrange("p t (c i) -> p c t i", i=RUN),
             )
-
-        h_rows = {}
-
-        def fetch(c, unit):
-            h_rows[c, unit] = stage.tile([P, PACK, CHUNK], BF16, name="h_rows")
-            nc.sync.dma_start(out=h_rows[c, unit][:].rearrange("p t w -> p (t w)"), in_=parking_place(c, unit))
-
-        hq_words, hq_scales = {}, {}
 
         def quantise_h(c, unit):
             hq_words[c, unit] = keep.tile([P, CHUNK], I32, name="hq_words_%d_%d" % (c, unit), align_bytes=64)
             hq_scales[c, unit] = keep.tile([P, CHUNK], U8, name="hq_scales_%d_%d" % (c, unit), align_bytes=64)
-            h_grouped = stage.tile([P, CHUNK, PACK], BF16, align_bytes=64)
-            nc.vector.tensor_copy(
-                out=h_grouped[:].rearrange("p (c i) t -> p c t i", i=4),
-                in_=h_rows[c, unit][:].rearrange("p t (c i) -> p c t i", i=4),
-            )
             nc.vector.quantize_mx(
                 out=hq_words[c, unit][:].bitcast(FP8X4),
                 scales=hq_scales[c, unit][:],
-                in_=h_grouped[:].rearrange("p w t -> p (w t)"),
+                in_=h_grouped[c, unit][:].rearrange("p w t -> p (w t)"),
             )
 
-        def gate_tile(c, i):
-            half, j = divmod(i, BLOCK)
-            y = sums.tile([P, CHUNK], F32, tag="sums")
-            for g in range(H_PASSES):
+        def gate_tile(c, s, first, width):
+            half, start = divmod(first, BANK)
+            y = sums.tile([P, width], F32, name="y", tag="sums")
+            for u in range(UNITS):
                 nc.tensor.matmul_mx(
                     out=y[:],
-                    lhsT=w2_words[half][:, g, P * j : P * (j + 1)].bitcast(FP8X4),
-                    lhsT_scale=w2_planes[PACK * g : P, P * i : P * (i + 1)],
-                    rhs=hq_words[c, g][:].bitcast(FP8X4),
-                    rhs_scale=hq_scales[c, g][:],
-                    start=(g == 0),
-                    stop=(g == H_PASSES - 1),
+                    lhsT=hq_words[c, u][:, P * s : P * (s + 1)].bitcast(FP8X4),
+                    lhsT_scale=hq_scales[c, u][:, P * s : P * (s + 1)],
+                    rhs=w2_words[half][:, u, start : start + width].bitcast(FP8X4),
+                    rhs_scale=w2_planes[PACK * u : P, first : first + width],
+                    start=(u == 0),
+                    stop=(u == UNITS - 1),
                 )
-            gate = gates.tile([P, CHUNK], F32)
-            nc.scalar.activation(
-                out=gate[:], in_=y[:], func=ACT.Sigmoid, bias=bias_cols[:, B2G_COL + i : B2G_COL + i + 1], scale=1.0
+            gate = results.tile([P, width], F32, name="gate")
+            nc.vector.tensor_tensor(
+                out=gate[:], in0=y[:], in1=b2g_all[:, first : first + width], op=ALU.add
             )
+            nc.scalar.activation(out=gate[:], in_=gate[:], func=ACT.Sigmoid)
             return gate
 
-        def finish_block(c, half, block):
-            banks = [flipped.tile([P, BANK], F32, name="gate_bank_%d" % s, tag="flipped") for s in range(TOKEN_TILES)]
-            for j in range(BLOCK):
-                for s in range(TOKEN_TILES):
-                    nc.tensor.transpose(
-                        out=banks[s][:, P * j : P * (j + 1)], in_=block[j][:, P * s : P * (s + 1)], identity=identity[:]
-                    )
-            for s in range(TOKEN_TILES):
-                result = results.tile([P, BANK], F32)
-                nc.vector.tensor_tensor(out=result[:], in0=banks[s][:], in1=values[c, half, s][:], op=ALU.mult)
-                first = CHUNK * c + P * s
-                nc.sync.dma_start(out=out_rows[first : first + P, BANK * half : BANK * (half + 1)], in_=result[:])
-
-        bias_rows_f32 = keep.tile([P, P], F32)
-        nc.vector.tensor_copy(out=bias_rows_f32[:], in_=bias_rows[:])
-
-        quantise_x(0)
-
-        bias_bank = flipped.tile([P, P], F32, tag="flipped")
-        nc.tensor.transpose(out=bias_bank[:], in_=bias_rows_f32[:], identity=identity[:])
-        bias_cols = keep.tile([P, P], F32)
-        nc.vector.tensor_copy(out=bias_cols[:], in_=bias_bank[:])
-        bv_all = keep.tile([P, D_MODEL], F32)
-        for half in range(HALVES):
-            bv_bank = flipped.tile([P, BANK], F32, tag="flipped")
-            nc.tensor.matmul(
-                out=bv_bank[:], lhsT=ones[:], rhs=bv_row[:, BANK * half : BANK * (half + 1)], start=True, stop=True
+        def finish_tile(c, s, first, width, gate):
+            half, start = divmod(first, BANK)
+            result = results.tile([P, width], F32, name="result")
+            engine = nc.gpsimd if half == 0 and (c, s) != (N_CHUNKS - 1, TOKEN_TILES - 1) else nc.vector
+            engine.tensor_tensor(
+                out=result[:], in0=gate[:], in1=values[c, half, s][:, start : start + width], op=ALU.mult
             )
-            nc.scalar.copy(out=bv_all[:, BANK * half : BANK * (half + 1)], in_=bv_bank[:])
+            row = CHUNK * c + P * s
+            nc.sync.dma_start(out=out_rows[row : row + P, first : first + width], in_=result[:])
 
-        w2_words = []
-        parked = []
+        bv_all = keep.tile([P, D_MODEL], F32)
+
+        def spread_bv(half):
+            bank = sums.tile([P, BANK], F32, tag="sums")
+            columns = slice(BANK * half, BANK * (half + 1))
+            nc.tensor.matmul(out=bank[:], lhsT=ones[:, 0:P], rhs=bv_row[:, columns], start=True, stop=True)
+            nc.scalar.copy(out=bv_all[:, columns], in_=bank[:])
+
+        for turn in range(WARM_UP):
+            idle = sums.tile([P, BANK], F32, tag="sums")
+            nc.tensor.matmul(out=idle[:], lhsT=ones[:, 0:P], rhs=ones[:], start=True, stop=True)
+
+        first = transpose_x(0, 0)
+        second = transpose_x(0, 1)
+        quantise_x(0, 0, first)
+        quantise_x(0, 1, second)
+        spread_bv(0)
+        value_tile(0, 0, 0)
+        value_tile(0, 0, 1)
+        spread_bv(1)
+        first = transpose_x(0, 2)
+        second = transpose_x(0, 3)
+        quantise_x(0, 2, first)
+        quantise_x(0, 3, second)
+        value_tile(0, 1, 0)
+        value_tile(0, 1, 1)
+        sort_w1_planes(0)
+        value_tile(0, 0, 2)
+        value_tile(0, 0, 3)
+        sort_w1_words(0)
+        value_tile(0, 1, 2)
+        value_tile(0, 1, 3)
+        first = transpose_x(1, 0)
+        second = transpose_x(1, 1)
+        quantise_x(1, 0, first)
+        quantise_x(1, 1, second)
+        sort_w1_planes(1)
+        sort_w1_words(1)
+
+        waiting_values = [(1, half, s) for s in range(TOKEN_TILES) for half in range(HALVES)]
+        since = 0
+        unit_no = 0
+        to_group, to_quantise = [], []
         for c in range(N_CHUNKS):
-            for unit in range(H_PASSES):
-                if len(parked) > ROUND_TRIP:
-                    quantise_h(*parked[0])
-                    parked = parked[1:]
-                if unit == H_PASSES - 1 and c + 1 < N_CHUNKS:
-                    quantise_x(c + 1)
-                h_cols = stage.tile([P, UNIT_TILES, CHUNK], BF16)
-                for j in range(UNIT_TILES):
-                    hidden_tile(c, unit, j, h_cols)
-                    v, place = divmod(UNIT_TILES * unit + j, H_PER_VALUE)
-                    if place == H_PER_VALUE - 1:
-                        value_tile(c, v // TOKEN_TILES, v % TOKEN_TILES)
-                park(c, unit, h_cols)
-                if unit > 0:
-                    fetch(c, unit - 1)
-                parked.append((c, unit))
-                if not w2_words:
-                    load_planes(w2_planes, W2g_scales)
-                    w2_words.extend(load_words(W2g_words, half, "w2") for half in range(HALVES))
-            for v in range(HIDDEN_TILES // H_PER_VALUE, VALUE_TILES):
-                value_tile(c, v // TOKEN_TILES, v % TOKEN_TILES)
-            fetch(c, H_PASSES - 1)
+            for unit in range(UNITS):
+                for t in range(PACK):
+                    hidden_tile(c, unit, t)
+                    since += 1
+                    if unit_no > 0 and since >= 3 and waiting_values:
+                        value_tile(*waiting_values[0])
+                        waiting_values = waiting_values[1:]
+                        since = 0
+                    if t == 1 and to_group:
+                        group_h(*to_group[0])
+                        to_quantise.append(to_group[0])
+                        to_group = to_group[1:]
+                    if t == 2 and to_quantise:
+                        quantise_h(*to_quantise[0])
+                        to_quantise = to_quantise[1:]
+                to_group.append((c, unit))
+                if unit_no == 0:
+                    sort_w1_planes(2)
+                    first = transpose_x(1, 2)
+                    second = transpose_x(1, 3)
+                    quantise_x(1, 2, first)
+                    quantise_x(1, 3, second)
+                    sort_w1_words(2)
+                unit_no += 1
+        for late in waiting_values:
+            value_tile(*late)
 
-        block = []
-        for n in range(N_CHUNKS * GATE_TILES):
-            c, i = divmod(n, GATE_TILES)
-            block.append(gate_tile(c, i))
-            if len(block) == BLOCK + LAG:
-                for late in parked:
-                    quantise_h(*late)
-                parked = []
-                done = (n - LAG) // BLOCK
-                finish_block(done // HALVES, done % HALVES, block[:BLOCK])
-                block = block[BLOCK:]
-        finish_block(N_CHUNKS - 1, HALVES - 1, block)
+        gates = []
+        for c in range(N_CHUNKS):
+            for s in range(TOKEN_TILES):
+                for half in range(HALVES):
+                    if (c, s, half) == (0, 1, 0):
+                        group_h(*to_group[0])
+                    if (c, s, half) == (0, 3, 0):
+                        quantise_h(*to_group[0])
+                    pieces = 2 if (c, s, half) == (N_CHUNKS - 1, TOKEN_TILES - 1, HALVES - 1) else 1
+                    for piece in range(pieces):
+                        width = BANK // pieces
+                        first = BANK * half + width * piece
+                        gates.append((c, s, first, width, gate_tile(c, s, first, width)))
+                        if len(gates) > 2:
+                            finish_tile(*gates[0])
+                            gates = gates[1:]
+        for late in gates:
+            finish_tile(*late)

@@ -25,7 +25,10 @@ X_PASSES = D_MODEL // K_PASS
 UNITS = D_HIDDEN // K_PASS
 HALVES = D_MODEL // BANK
 QUADRANTS = 4
-SCALAR_GROUPS = ((0, 1), (1, 2))
+HIDDEN_TILES = D_HIDDEN // P
+VALUE_TILES = TOKEN_TILES * HALVES
+OUT_TILES = TOKENS // P * HALVES
+LAG = 3
 WARM_UP = 4
 RUN = 4
 
@@ -47,11 +50,11 @@ def tile_selectivemixing_pa_kernel(
         sums = ctx.enter_context(tc.psum_pool(name="sums", bufs=6))
         flipped = ctx.enter_context(tc.psum_pool(name="flipped", bufs=2))
 
+        ones = keep.tile([P, BANK], BF16)
+        bv_row = keep.tile([P, D_MODEL], BF16)
         wv_planes = keep.tile([P, D_MODEL], U8, align_bytes=64)
         w1_planes = keep.tile([P, D_HIDDEN], U8, align_bytes=64)
         w2_planes = keep.tile([P, D_MODEL], U8, align_bytes=64)
-        bv_row = keep.tile([P, D_MODEL], BF16)
-        ones = keep.tile([P, BANK], BF16)
         nc.vector.memset(ones[:], 1.0)
         nc.vector.memset(bv_row[:].bitcast(I32), 0)
         nc.vector.memset(wv_planes[:].bitcast(I32), 0)
@@ -68,12 +71,15 @@ def tile_selectivemixing_pa_kernel(
                     in_=scales[:, 4 * quadrant : 4 * quadrant + 4, :].bitcast(I32),
                 )
 
-        def load_words(words, piece, name):
+        def load_words(words, piece, name, loads=1):
             loaded = keep.tile([P, words.shape[0], BANK], I32, name="%s_%d" % (name, piece), align_bytes=64)
-            nc.sync.dma_start(
-                out=loaded[:],
-                in_=words.rearrange("g p n t -> p g (n t)").bitcast(I32)[:, :, BANK * piece : BANK * (piece + 1)],
-            )
+            width = BANK // loads
+            for start in range(0, BANK, width):
+                first = BANK * piece + start
+                nc.sync.dma_start(
+                    out=loaded[:, :, start : start + width],
+                    in_=words.rearrange("g p n t -> p g (n t)").bitcast(I32)[:, :, first : first + width],
+                )
             return loaded
 
         x_tiles = {}
@@ -87,7 +93,6 @@ def tile_selectivemixing_pa_kernel(
             for i in range(count):
                 x_tiles[c, s + i] = loaded[:, i, :]
 
-        b1_cols = keep.tile([P, UNITS * PACK], BF16)
         nc.scalar.dma_start(out=bv_row[0:1, :], in_=bv.rearrange("(o d) -> o d", o=1))
         warm = keep.tile([P, 1], F32)
         nc.scalar.activation(out=warm[:], in_=ones[:, 0:1], func=ACT.Silu)
@@ -99,6 +104,7 @@ def tile_selectivemixing_pa_kernel(
         wv_words.append(load_words(Wv_words, 1, "wv"))
         load_planes(w1_planes, W1_scales)
         w1_words = [load_words(W1_words, 0, "w1")]
+        b1_cols = keep.tile([P, UNITS * PACK], BF16)
         nc.sync.dma_start(
             out=b1_cols[:].rearrange("p (u t) -> p u t", t=PACK), in_=b1.rearrange("(u p t) -> p u t", p=P, t=PACK)
         )
@@ -117,7 +123,7 @@ def tile_selectivemixing_pa_kernel(
 
         def transpose_x(c, s):
             x_as_words = x_tiles[c, s].bitcast(F32)
-            bank = flipped.tile([P, X_PASSES, 2, P], F32, tag="flipped")
+            bank = flipped.tile([P, X_PASSES, 2, P], F32, name="x_bank", tag="flipped")
             for g in range(X_PASSES):
                 for u in range(2):
                     nc.tensor.transpose(
@@ -126,31 +132,39 @@ def tile_selectivemixing_pa_kernel(
                         identity=identity[:],
                     )
             grouped = stage.tile([P, X_PASSES, P, PACK], BF16, name="x_grouped", align_bytes=64)
+            grouped_words = grouped[:].rearrange("p g w t -> p (g w t)").bitcast(F32)
             nc.scalar.copy(
-                out=grouped[:].rearrange("p g w t -> p (g w t)").bitcast(F32).rearrange("p (g w u) -> p g w u", g=X_PASSES, u=2),
+                out=grouped_words.rearrange("p (g w u) -> p g w u", g=X_PASSES, u=2),
                 in_=bank[:].rearrange("p g u w -> p g w u"),
             )
             return grouped
 
         def quantise_x(c, s, grouped):
+            tokens = slice(P * s, P * (s + 1))
             for g in range(X_PASSES):
                 nc.vector.quantize_mx(
-                    out=xq_words[c][:, g, P * s : P * (s + 1)].bitcast(FP8X4),
-                    scales=xq_scales[c][:, g, P * s : P * (s + 1)],
+                    out=xq_words[c][:, g, tokens].bitcast(FP8X4),
+                    scales=xq_scales[c][:, g, tokens],
                     in_=grouped[:, g].rearrange("p w t -> p (w t)"),
                 )
 
-        w1_sorted = [keep.tile([P, X_PASSES, K_PASS], I32, name="w1_sorted_%d" % u, align_bytes=64) for u in range(UNITS)]
+        def prepare_x(c, s):
+            grouped = [transpose_x(c, s), transpose_x(c, s + 1)]
+            quantise_x(c, s, grouped[0])
+            quantise_x(c, s + 1, grouped[1])
+
+        w1_sorted = {}
         w1_sorted_planes = keep.tile([P, D_HIDDEN], U8, align_bytes=64)
 
-        def sort_w1_planes(unit):
+        def sort_planes(unit):
             columns = slice(K_PASS * unit, K_PASS * (unit + 1))
             nc.vector.tensor_copy(
                 out=w1_sorted_planes[:, columns].rearrange("p (t m) -> p m t", t=PACK),
                 in_=w1_planes[:, columns].rearrange("p (m t) -> p m t", t=PACK),
             )
 
-        def sort_w1_words(unit):
+        def sort_words(unit):
+            w1_sorted[unit] = keep.tile([P, X_PASSES, K_PASS], I32, name="w1_sorted_%d" % unit, align_bytes=64)
             for g in range(X_PASSES):
                 nc.vector.tensor_copy(
                     out=w1_sorted[unit][:, g, :].rearrange("p (t c i) -> p c t i", t=PACK, i=RUN),
@@ -162,7 +176,7 @@ def tile_selectivemixing_pa_kernel(
         def hidden_tile(c, unit, t):
             if t == 0:
                 h_cols[c, unit] = stage.tile([P, PACK, CHUNK], BF16, name="h_cols")
-            z = sums.tile([P, CHUNK], F32, tag="sums")
+            z = sums.tile([P, CHUNK], F32, name="z", tag="sums")
             first = K_PASS * unit + P * t
             for g in range(X_PASSES):
                 nc.tensor.matmul_mx(
@@ -179,31 +193,11 @@ def tile_selectivemixing_pa_kernel(
                 out=h_cols[c, unit][:, t, :], in_=z[:], func=ACT.Silu, bias=b1_cols[:, column : column + 1], scale=1.0
             )
 
-        values = {}
-
-        def value_tile(c, half, s):
-            v = sums.tile([P, BANK], F32, tag="sums")
-            for g in range(X_PASSES):
-                nc.tensor.matmul_mx(
-                    out=v[:],
-                    lhsT=xq_words[c][:, g, P * s : P * (s + 1)].bitcast(FP8X4),
-                    lhsT_scale=xq_scales[c][:, g, P * s : P * (s + 1)],
-                    rhs=wv_words[half][:, g, :].bitcast(FP8X4),
-                    rhs_scale=wv_planes[PACK * g : P, BANK * half : BANK * (half + 1)],
-                    start=(g == 0),
-                    stop=(g == X_PASSES - 1),
-                )
-            values[c, half, s] = keep.tile([P, BANK], F32, name="value_%d_%d_%d" % (c, half, s))
-            nc.vector.tensor_tensor(
-                out=values[c, half, s][:], in0=v[:], in1=bv_all[:, BANK * half : BANK * (half + 1)], op=ALU.add
-            )
-
         hq_words, hq_scales, h_grouped = {}, {}, {}
 
         def group_h(c, unit):
             h_grouped[c, unit] = stage.tile([P, CHUNK, PACK], BF16, name="h_grouped", align_bytes=64)
-            copy = nc.scalar.copy if (c, unit) in SCALAR_GROUPS else nc.vector.tensor_copy
-            copy(
+            nc.vector.tensor_copy(
                 out=h_grouped[c, unit][:].rearrange("p (c i) t -> p c t i", i=RUN),
                 in_=h_cols[c, unit][:].rearrange("p t (c i) -> p c t i", i=RUN),
             )
@@ -217,7 +211,29 @@ def tile_selectivemixing_pa_kernel(
                 in_=h_grouped[c, unit][:].rearrange("p w t -> p (w t)"),
             )
 
-        def gate_tile(c, s, first, width):
+        values = {}
+
+        def value_tile(c, s, half, start=0, width=BANK):
+            first = BANK * half + start
+            if start == 0:
+                values[c, s, half] = keep.tile([P, BANK], F32, name="value_%d_%d_%d" % (c, s, half))
+            v = sums.tile([P, width], F32, name="v", tag="sums")
+            for g in range(X_PASSES):
+                nc.tensor.matmul_mx(
+                    out=v[:],
+                    lhsT=xq_words[c][:, g, P * s : P * (s + 1)].bitcast(FP8X4),
+                    lhsT_scale=xq_scales[c][:, g, P * s : P * (s + 1)],
+                    rhs=wv_words[half][:, g, start : start + width].bitcast(FP8X4),
+                    rhs_scale=wv_planes[PACK * g : P, first : first + width],
+                    start=(g == 0),
+                    stop=(g == X_PASSES - 1),
+                )
+            nc.vector.tensor_tensor(
+                out=values[c, s, half][:, start : start + width], in0=v[:], in1=bv_all[:, first : first + width], op=ALU.add
+            )
+
+        def gate_tile(n, first, width):
+            c, s = divmod(n // HALVES, TOKEN_TILES)
             half, start = divmod(first, BANK)
             y = sums.tile([P, width], F32, name="y", tag="sums")
             for u in range(UNITS):
@@ -231,108 +247,93 @@ def tile_selectivemixing_pa_kernel(
                     stop=(u == UNITS - 1),
                 )
             gate = results.tile([P, width], F32, name="gate")
-            nc.vector.tensor_tensor(
-                out=gate[:], in0=y[:], in1=b2g_all[:, first : first + width], op=ALU.add
-            )
+            nc.vector.tensor_tensor(out=gate[:], in0=y[:], in1=b2g_all[:, first : first + width], op=ALU.add)
             nc.scalar.activation(out=gate[:], in_=gate[:], func=ACT.Sigmoid)
             return gate
 
-        def finish_tile(c, s, first, width, gate):
+        def finish_tile(n, first, width, gate):
+            c, s = divmod(n // HALVES, TOKEN_TILES)
             half, start = divmod(first, BANK)
             result = results.tile([P, width], F32, name="result")
-            engine = nc.gpsimd if half == 0 and (c, s) != (N_CHUNKS - 1, TOKEN_TILES - 1) else nc.vector
+            engine = nc.gpsimd if n % 2 == 0 and n < OUT_TILES - 2 else nc.vector
             engine.tensor_tensor(
-                out=result[:], in0=gate[:], in1=values[c, half, s][:, start : start + width], op=ALU.mult
+                out=result[:], in0=gate[:], in1=values[c, s, half][:, start : start + width], op=ALU.mult
             )
             row = CHUNK * c + P * s
             nc.sync.dma_start(out=out_rows[row : row + P, first : first + width], in_=result[:])
 
+        for turn in range(WARM_UP):
+            idle = sums.tile([P, BANK], F32, name="idle", tag="sums")
+            nc.tensor.matmul(out=idle[:], lhsT=ones[:, 0:P], rhs=ones[:], start=True, stop=True)
+
         bv_all = keep.tile([P, D_MODEL], F32)
 
         def spread_bv(half):
-            bank = sums.tile([P, BANK], F32, tag="sums")
+            bank = sums.tile([P, BANK], F32, name="bv_bank", tag="sums")
             columns = slice(BANK * half, BANK * (half + 1))
             nc.tensor.matmul(out=bank[:], lhsT=ones[:, 0:P], rhs=bv_row[:, columns], start=True, stop=True)
             nc.scalar.copy(out=bv_all[:, columns], in_=bank[:])
 
-        for turn in range(WARM_UP):
-            idle = sums.tile([P, BANK], F32, tag="sums")
-            nc.tensor.matmul(out=idle[:], lhsT=ones[:, 0:P], rhs=ones[:], start=True, stop=True)
-
-        first = transpose_x(0, 0)
-        second = transpose_x(0, 1)
-        quantise_x(0, 0, first)
-        quantise_x(0, 1, second)
+        prepare_x(0, 0)
         spread_bv(0)
         value_tile(0, 0, 0)
-        value_tile(0, 0, 1)
-        spread_bv(1)
-        first = transpose_x(0, 2)
-        second = transpose_x(0, 3)
-        quantise_x(0, 2, first)
-        quantise_x(0, 3, second)
         value_tile(0, 1, 0)
+        spread_bv(1)
+        prepare_x(0, 2)
+        value_tile(0, 0, 1)
         value_tile(0, 1, 1)
-        sort_w1_planes(0)
-        value_tile(0, 0, 2)
-        value_tile(0, 0, 3)
-        sort_w1_words(0)
-        value_tile(0, 1, 2)
-        value_tile(0, 1, 3)
-        first = transpose_x(1, 0)
-        second = transpose_x(1, 1)
-        quantise_x(1, 0, first)
-        quantise_x(1, 1, second)
-        sort_w1_planes(1)
-        sort_w1_words(1)
+        sort_planes(0)
+        value_tile(0, 2, 0)
+        value_tile(0, 3, 0)
+        sort_words(0)
+        value_tile(0, 2, 1)
+        value_tile(0, 3, 1)
+        prepare_x(1, 0)
+        sort_planes(1)
+        sort_words(1)
 
-        waiting_values = [(1, half, s) for s in range(TOKEN_TILES) for half in range(HALVES)]
-        since = 0
-        unit_no = 0
-        to_group, to_quantise = [], []
+        values_left = [(1, s, half) for s in range(TOKEN_TILES) for half in range(HALVES)]
+        steps = []
+        place = 0
+
+        def step_on(place):
+            for due, step, arguments in steps:
+                if due == place:
+                    step(*arguments)
+            return place + 1
+
         for c in range(N_CHUNKS):
             for unit in range(UNITS):
                 for t in range(PACK):
                     hidden_tile(c, unit, t)
-                    since += 1
-                    if unit_no > 0 and since >= 3 and waiting_values:
-                        value_tile(*waiting_values[0])
-                        waiting_values = waiting_values[1:]
-                        since = 0
-                    if t == 1 and to_group:
-                        group_h(*to_group[0])
-                        to_quantise.append(to_group[0])
-                        to_group = to_group[1:]
-                    if t == 2 and to_quantise:
-                        quantise_h(*to_quantise[0])
-                        to_quantise = to_quantise[1:]
-                to_group.append((c, unit))
-                if unit_no == 0:
-                    sort_w1_planes(2)
-                    first = transpose_x(1, 2)
-                    second = transpose_x(1, 3)
-                    quantise_x(1, 2, first)
-                    quantise_x(1, 3, second)
-                    sort_w1_words(2)
-                unit_no += 1
-        for late in waiting_values:
+                    if t == PACK - 1:
+                        last = (c, unit) == (N_CHUNKS - 1, UNITS - 1)
+                        steps.append((place + (1 if last else 1), group_h, (c, unit)))
+                        steps.append((place + (3 if last else 4), quantise_h, (c, unit)))
+                    place = step_on(place)
+                    behind = (c * UNITS + unit) * PACK + t + 1 - PACK
+                    if behind * VALUE_TILES // (N_CHUNKS * HIDDEN_TILES - PACK) > VALUE_TILES - len(values_left):
+                        value_tile(*values_left[0])
+                        values_left = values_left[1:]
+                        place = step_on(place)
+                if (c, unit) == (0, 0):
+                    sort_planes(2)
+                    prepare_x(1, 2)
+                    sort_words(2)
+        for late in values_left:
             value_tile(*late)
+            place = step_on(place)
 
         gates = []
-        for c in range(N_CHUNKS):
-            for s in range(TOKEN_TILES):
-                for half in range(HALVES):
-                    if (c, s, half) == (0, 1, 0):
-                        group_h(*to_group[0])
-                    if (c, s, half) == (0, 3, 0):
-                        quantise_h(*to_group[0])
-                    pieces = 2 if (c, s, half) == (N_CHUNKS - 1, TOKEN_TILES - 1, HALVES - 1) else 1
-                    for piece in range(pieces):
-                        width = BANK // pieces
-                        first = BANK * half + width * piece
-                        gates.append((c, s, first, width, gate_tile(c, s, first, width)))
-                        if len(gates) > 2:
-                            finish_tile(*gates[0])
-                            gates = gates[1:]
+        for n in range(OUT_TILES):
+            pieces = 2 if n == OUT_TILES - 1 else 1
+            width = BANK // pieces
+            for piece in range(pieces):
+                first = BANK * (n % HALVES) + width * piece
+                gates.append((n, first, width, gate_tile(n, first, width)))
+                if len(gates) > LAG:
+                    finish_tile(*gates[0])
+                    gates = gates[1:]
+            place = step_on(place)
         for late in gates:
             finish_tile(*late)

@@ -29,7 +29,7 @@ HIDDEN_TILES = D_HIDDEN // P
 VALUE_TILES = TOKEN_TILES * HALVES
 OUT_TILES = TOKENS // P * HALVES
 LAG = 3
-WARM_UP = 4
+WARM_UP = 7
 RUN = 4
 
 FLOPS = 2 * TOKENS * (D_MODEL * D_HIDDEN + D_HIDDEN * D_MODEL + D_MODEL * D_MODEL)
@@ -158,7 +158,7 @@ def tile_selectivemixing_pa_kernel(
 
         def sort_planes(unit):
             columns = slice(K_PASS * unit, K_PASS * (unit + 1))
-            nc.vector.tensor_copy(
+            nc.gpsimd.tensor_copy(
                 out=w1_sorted_planes[:, columns].rearrange("p (t m) -> p m t", t=PACK),
                 in_=w1_planes[:, columns].rearrange("p (m t) -> p m t", t=PACK),
             )
@@ -262,9 +262,12 @@ def tile_selectivemixing_pa_kernel(
             row = CHUNK * c + P * s
             nc.sync.dma_start(out=out_rows[row : row + P, first : first + width], in_=result[:])
 
-        for turn in range(WARM_UP):
-            idle = sums.tile([P, BANK], F32, name="idle", tag="sums")
-            nc.tensor.matmul(out=idle[:], lhsT=ones[:, 0:P], rhs=ones[:], start=True, stop=True)
+        def warm_up(count):
+            for turn in range(count):
+                idle = sums.tile([P, BANK], F32, name="idle", tag="sums")
+                nc.tensor.matmul(out=idle[:], lhsT=ones[:, 0:P], rhs=ones[:], start=True, stop=True)
+
+        warm_up(WARM_UP)
 
         bv_all = keep.tile([P, D_MODEL], F32)
 
@@ -276,6 +279,7 @@ def tile_selectivemixing_pa_kernel(
 
         prepare_x(0, 0)
         spread_bv(0)
+        warm_up(2)
         value_tile(0, 0, 0)
         value_tile(0, 1, 0)
         spread_bv(1)

from contextlib import ExitStack

import concourse.mybir as mybir
from concourse.masks import make_identity

F32 = mybir.dt.float32
BF16 = mybir.dt.bfloat16
I32 = mybir.dt.int32
U8 = mybir.dt.uint8
FP8X4 = mybir.dt.float8_e4m3fn_x4
ACT = mybir.ActivationFunctionType
ALU = mybir.AluOpType

P = 128
PACK = 4
K_PASS = P * PACK
BANK = 512
TOKENS = 1024
D_MODEL = 1024
D_HIDDEN = 1536
CHUNK = BANK
N_CHUNKS = TOKENS // CHUNK
TOKEN_TILES = CHUNK // P
X_PASSES = D_MODEL // K_PASS
UNITS = D_HIDDEN // K_PASS
HALVES = D_MODEL // BANK
QUADRANTS = 4
HIDDEN_TILES = D_HIDDEN // P
VALUE_TILES = TOKEN_TILES * HALVES
OUT_TILES = TOKENS // P * HALVES
LAG = 3
WARM_UP = 7
RUN = 4

FLOPS = 2 * TOKENS * (D_MODEL * D_HIDDEN + D_HIDDEN * D_MODEL + D_MODEL * D_MODEL)


def tile_selectivemixing_pa_kernel(
    tc, x, W1_words, W1_scales, b1, W2g_words, W2g_scales, b2g, Wv_words, Wv_scales, bv, out
):
    nc = tc.nc
    x_rows = x.rearrange("b l d -> (b l) d")
    out_rows = out.rearrange("b l d -> (b l) d")

    with ExitStack() as ctx:
        ctx.enter_context(tc.manual_schedule())
        keep = ctx.enter_context(tc.tile_pool(name="keep", bufs=1))
        stage = ctx.enter_context(tc.tile_pool(name="stage", bufs=4))
        results = ctx.enter_context(tc.tile_pool(name="results", bufs=6))
        sums = ctx.enter_context(tc.psum_pool(name="sums", bufs=6))
        flipped = ctx.enter_context(tc.psum_pool(name="flipped", bufs=2))

        ones = keep.tile([P, BANK], BF16)
        bv_row = keep.tile([P, D_MODEL], BF16)
        wv_planes = keep.tile([P, D_MODEL], U8, align_bytes=64)
        w1_planes = keep.tile([P, D_HIDDEN], U8, align_bytes=64)
        w2_planes = keep.tile([P, D_MODEL], U8, align_bytes=64)
        nc.vector.memset(ones[:], 1.0)
        nc.vector.memset(bv_row[:].bitcast(I32), 0)
        nc.vector.memset(wv_planes[:].bitcast(I32), 0)
        nc.vector.memset(w1_planes[:].bitcast(I32), 0)
        nc.vector.memset(w2_planes[:].bitcast(I32), 0)
        identity = keep.tile([P, P], F32)
        make_identity(nc, identity[:])

        def load_planes(planes, scales):
            rows = PACK * scales.shape[0]
            for quadrant in range(QUADRANTS):
                nc.sync.dma_start(
                    out=planes[32 * quadrant : 32 * quadrant + rows, :].bitcast(I32),
                    in_=scales[:, 4 * quadrant : 4 * quadrant + 4, :].bitcast(I32),
                )

        def load_words(words, piece, name, loads=1):
            loaded = keep.tile([P, words.shape[0], BANK], I32, name="%s_%d" % (name, piece), align_bytes=64)
            width = BANK // loads
            for start in range(0, BANK, width):
                first = BANK * piece + start
                nc.sync.dma_start(
                    out=loaded[:, :, start : start + width],
                    in_=words.rearrange("g p n t -> p g (n t)").bitcast(I32)[:, :, first : first + width],
                )
            return loaded

        x_tiles = {}

        def load_x(c, s, count):
            loaded = keep.tile([P, count, D_MODEL], BF16, name="x_%d_%d" % (c, s))
            first = CHUNK * c + P * s
            nc.sync.dma_start(
                out=loaded[:], in_=x_rows[first : first + P * count, :].rearrange("(s p) d -> p s d", p=P)
            )
            for i in range(count):
                x_tiles[c, s + i] = loaded[:, i, :]

        nc.scalar.dma_start(out=bv_row[0:1, :], in_=bv.rearrange("(o d) -> o d", o=1))
        warm = keep.tile([P, 1], F32)
        nc.scalar.activation(out=warm[:], in_=ones[:, 0:1], func=ACT.Silu)
        load_x(0, 0, 1)
        load_x(0, 1, 1)
        load_planes(wv_planes, Wv_scales)
        wv_words = [load_words(Wv_words, 0, "wv")]
        load_x(0, 2, 2)
        wv_words.append(load_words(Wv_words, 1, "wv"))
        load_planes(w1_planes, W1_scales)
        w1_words = [load_words(W1_words, 0, "w1")]
        b1_cols = keep.tile([P, UNITS * PACK], BF16)
        nc.sync.dma_start(
            out=b1_cols[:].rearrange("p (u t) -> p u t", t=PACK), in_=b1.rearrange("(u p t) -> p u t", p=P, t=PACK)
        )
        load_x(1, 0, 2)
        load_x(1, 2, 2)
        w1_words.extend(load_words(W1_words, unit, "w1") for unit in range(1, UNITS))
        load_planes(w2_planes, W2g_scales)
        w2_words = [load_words(W2g_words, half, "w2") for half in range(HALVES)]
        b2g_all = keep.tile([P, D_MODEL], BF16)
        nc.sync.dma_start(out=b2g_all[:], in_=b2g.partition_broadcast(P))

        xq_words, xq_scales = {}, {}
        for c in range(N_CHUNKS):
            xq_words[c] = keep.tile([P, X_PASSES, CHUNK], I32, name="xq_words_%d" % c, align_bytes=64)
            xq_scales[c] = keep.tile([P, X_PASSES, CHUNK], U8, name="xq_scales_%d" % c, align_bytes=64)

        def transpose_x(c, s):
            x_as_words = x_tiles[c, s].bitcast(F32)
            bank = flipped.tile([P, X_PASSES, 2, P], F32, name="x_bank", tag="flipped")
            for g in range(X_PASSES):
                for u in range(2):
                    nc.tensor.transpose(
                        out=bank[:, g, u, :],
                        in_=x_as_words[:, 2 * P * g + u : 2 * P * (g + 1) : 2],
                        identity=identity[:],
                    )
            grouped = stage.tile([P, X_PASSES, P, PACK], BF16, name="x_grouped", align_bytes=64)
            grouped_words = grouped[:].rearrange("p g w t -> p (g w t)").bitcast(F32)
            nc.scalar.copy(
                out=grouped_words.rearrange("p (g w u) -> p g w u", g=X_PASSES, u=2),
                in_=bank[:].rearrange("p g u w -> p g w u"),
            )
            return grouped

        def quantise_x(c, s, grouped):
            tokens = slice(P * s, P * (s + 1))
            for g in range(X_PASSES):
                nc.vector.quantize_mx(
                    out=xq_words[c][:, g, tokens].bitcast(FP8X4),
                    scales=xq_scales[c][:, g, tokens],
                    in_=grouped[:, g].rearrange("p w t -> p (w t)"),
                )

        def prepare_x(c, s):
            grouped = [transpose_x(c, s), transpose_x(c, s + 1)]
            quantise_x(c, s, grouped[0])
            quantise_x(c, s + 1, grouped[1])

        w1_sorted = {}
        w1_sorted_planes = keep.tile([P, D_HIDDEN], U8, align_bytes=64)

        def sort_planes(unit):
            columns = slice(K_PASS * unit, K_PASS * (unit + 1))
            nc.gpsimd.tensor_copy(
                out=w1_sorted_planes[:, columns].rearrange("p (t m) -> p m t", t=PACK),
                in_=w1_planes[:, columns].rearrange("p (m t) -> p m t", t=PACK),
            )

        def sort_words(unit):
            w1_sorted[unit] = keep.tile([P, X_PASSES, K_PASS], I32, name="w1_sorted_%d" % unit, align_bytes=64)
            for g in range(X_PASSES):
                nc.vector.tensor_copy(
                    out=w1_sorted[unit][:, g, :].rearrange("p (t c i) -> p c t i", t=PACK, i=RUN),
                    in_=w1_words[unit][:, g, :].rearrange("p (c i t) -> p c t i", t=PACK, i=RUN),
                )

        h_cols = {}

        def hidden_tile(c, unit, t):
            if t == 0:
                h_cols[c, unit] = stage.tile([P, PACK, CHUNK], BF16, name="h_cols")
            z = sums.tile([P, CHUNK], F32, name="z", tag="sums")
            first = K_PASS * unit + P * t
            for g in range(X_PASSES):
                nc.tensor.matmul_mx(
                    out=z[:],
                    lhsT=w1_sorted[unit][:, g, P * t : P * (t + 1)].bitcast(FP8X4),
                    lhsT_scale=w1_sorted_planes[PACK * g : P, first : first + P],
                    rhs=xq_words[c][:, g, :].bitcast(FP8X4),
                    rhs_scale=xq_scales[c][:, g, :],
                    start=(g == 0),
                    stop=(g == X_PASSES - 1),
                )
            column = PACK * unit + t
            nc.scalar.activation(
                out=h_cols[c, unit][:, t, :], in_=z[:], func=ACT.Silu, bias=b1_cols[:, column : column + 1], scale=1.0
            )

        hq_words, hq_scales, h_grouped = {}, {}, {}

        def group_h(c, unit):
            h_grouped[c, unit] = stage.tile([P, CHUNK, PACK], BF16, name="h_grouped", align_bytes=64)
            nc.vector.tensor_copy(
                out=h_grouped[c, unit][:].rearrange("p (c i) t -> p c t i", i=RUN),
                in_=h_cols[c, unit][:].rearrange("p t (c i) -> p c t i", i=RUN),
            )

        def quantise_h(c, unit):
            hq_words[c, unit] = keep.tile([P, CHUNK], I32, name="hq_words_%d_%d" % (c, unit), align_bytes=64)
            hq_scales[c, unit] = keep.tile([P, CHUNK], U8, name="hq_scales_%d_%d" % (c, unit), align_bytes=64)
            nc.vector.quantize_mx(
                out=hq_words[c, unit][:].bitcast(FP8X4),
                scales=hq_scales[c, unit][:],
                in_=h_grouped[c, unit][:].rearrange("p w t -> p (w t)"),
            )

        values = {}

        def value_tile(c, s, half, start=0, width=BANK):
            first = BANK * half + start
            if start == 0:
                values[c, s, half] = keep.tile([P, BANK], F32, name="value_%d_%d_%d" % (c, s, half))
            v = sums.tile([P, width], F32, name="v", tag="sums")
            for g in range(X_PASSES):
                nc.tensor.matmul_mx(
                    out=v[:],
                    lhsT=xq_words[c][:, g, P * s : P * (s + 1)].bitcast(FP8X4),
                    lhsT_scale=xq_scales[c][:, g, P * s : P * (s + 1)],
                    rhs=wv_words[half][:, g, start : start + width].bitcast(FP8X4),
                    rhs_scale=wv_planes[PACK * g : P, first : first + width],
                    start=(g == 0),
                    stop=(g == X_PASSES - 1),
                )
            nc.vector.tensor_tensor(
                out=values[c, s, half][:, start : start + width], in0=v[:], in1=bv_all[:, first : first + width], op=ALU.add
            )

        def gate_tile(n, first, width):
            c, s = divmod(n // HALVES, TOKEN_TILES)
            half, start = divmod(first, BANK)
            y = sums.tile([P, width], F32, name="y", tag="sums")
            for u in range(UNITS):
                nc.tensor.matmul_mx(
                    out=y[:],
                    lhsT=hq_words[c, u][:, P * s : P * (s + 1)].bitcast(FP8X4),
                    lhsT_scale=hq_scales[c, u][:, P * s : P * (s + 1)],
                    rhs=w2_words[half][:, u, start : start + width].bitcast(FP8X4),
                    rhs_scale=w2_planes[PACK * u : P, first : first + width],
                    start=(u == 0),
                    stop=(u == UNITS - 1),
                )
            gate = results.tile([P, width], F32, name="gate")
            nc.vector.tensor_tensor(out=gate[:], in0=y[:], in1=b2g_all[:, first : first + width], op=ALU.add)
            nc.scalar.activation(out=gate[:], in_=gate[:], func=ACT.Sigmoid)
            return gate

        def finish_tile(n, first, width, gate):
            c, s = divmod(n // HALVES, TOKEN_TILES)
            half, start = divmod(first, BANK)
            result = results.tile([P, width], F32, name="result")
            engine = nc.gpsimd if n % 2 == 0 and n < OUT_TILES - 2 else nc.vector
            engine.tensor_tensor(
                out=result[:], in0=gate[:], in1=values[c, s, half][:, start : start + width], op=ALU.mult
            )
            row = CHUNK * c + P * s
            nc.sync.dma_start(out=out_rows[row : row + P, first : first + width], in_=result[:])

        def warm_up(count):
            for turn in range(count):
                idle = sums.tile([P, BANK], F32, name="idle", tag="sums")
                nc.tensor.matmul(out=idle[:], lhsT=ones[:, 0:P], rhs=ones[:], start=True, stop=True)

        warm_up(WARM_UP)

        bv_all = keep.tile([P, D_MODEL], F32)

        def spread_bv(half):
            bank = sums.tile([P, BANK], F32, name="bv_bank", tag="sums")
            columns = slice(BANK * half, BANK * (half + 1))
            nc.tensor.matmul(out=bank[:], lhsT=ones[:, 0:P], rhs=bv_row[:, columns], start=True, stop=True)
            nc.scalar.copy(out=bv_all[:, columns], in_=bank[:])

        prepare_x(0, 0)
        spread_bv(0)
        warm_up(2)
        value_tile(0, 0, 0)
        value_tile(0, 1, 0)
        spread_bv(1)
        prepare_x(0, 2)
        value_tile(0, 0, 1)
        value_tile(0, 1, 1)
        sort_planes(0)
        value_tile(0, 2, 0)
        value_tile(0, 3, 0)
        sort_words(0)
        value_tile(0, 2, 1)
        value_tile(0, 3, 1)
        prepare_x(1, 0)
        sort_planes(1)
        sort_words(1)

        values_left = [(1, s, half) for s in range(TOKEN_TILES) for half in range(HALVES)]
        steps = []
        place = 0

        def step_on(place):
            for due, step, arguments in steps:
                if due == place:
                    step(*arguments)
            return place + 1

        for c in range(N_CHUNKS):
            for unit in range(UNITS):
                for t in range(PACK):
                    hidden_tile(c, unit, t)
                    if t == PACK - 1:
                        last = (c, unit) == (N_CHUNKS - 1, UNITS - 1)
                        steps.append((place + (1 if last else 1), group_h, (c, unit)))
                        steps.append((place + (3 if last else 4), quantise_h, (c, unit)))
                    place = step_on(place)
                    behind = (c * UNITS + unit) * PACK + t + 1 - PACK
                    if behind * VALUE_TILES // (N_CHUNKS * HIDDEN_TILES - PACK) > VALUE_TILES - len(values_left):
                        value_tile(*values_left[0])
                        values_left = values_left[1:]
                        place = step_on(place)
                if (c, unit) == (0, 0):
                    sort_planes(2)
                    prepare_x(1, 2)
                    sort_words(2)
        for late in values_left:
            value_tile(*late)
            place = step_on(place)

        gates = []
        for n in range(OUT_TILES):
            pieces = 2 if n == OUT_TILES - 1 else 1
            width = BANK // pieces
            for piece in range(pieces):
                first = BANK * (n % HALVES) + width * piece
                gates.append((n, first, width, gate_tile(n, first, width)))
                if len(gates) > LAG:
                    finish_tile(*gates[0])
                    gates = gates[1:]
            place = step_on(place)
        for late in gates:
            finish_tile(*late)
